import numpy as np
import ml_dtypes


BF16 = ml_dtypes.bfloat16


def bf(x):
    return np.asarray(x, np.float32).astype(BF16)


def f64(x):
    return np.asarray(x).astype(np.float64)


E2M1 = np.array([0.0, 0.5, 1.0, 1.5, 2.0, 3.0, 4.0, 6.0, -0.0, -0.5, -1.0, -1.5, -2.0, -3.0, -4.0, -6.0])


def pack_weight(w, fmt):
    k, n = w.shape
    w = f64(bf(w)).reshape(k // 32, 32, n)
    amax = np.abs(w).max(1)
    if fmt == "e4m3":
        byte = np.frexp(amax)[1] - 1 + 127 - 7
    else:
        mant, ex = np.frexp(amax / 6.0)
        byte = np.where(mant > 0.5, ex, ex - 1) + 127
    byte = np.clip(np.where(amax > 0, byte, 1), 1, 254)
    scaled = (w * np.exp2(127.0 - byte)[:, None, :]).reshape(k, n).astype(np.float32)
    by_word = np.ascontiguousarray(scaled.reshape(k // 512, 128, 4, n).transpose(0, 1, 3, 2))
    if fmt == "e4m3":
        words = by_word.astype(ml_dtypes.float8_e4m3fn).view(np.uint8)
    else:
        c = by_word.astype(ml_dtypes.float4_e2m1fn).view(np.uint8) & 0xF
        words = c[..., 0::2] | (c[..., 1::2] << 4)
    return np.ascontiguousarray(words), np.ascontiguousarray(byte.astype(np.uint8).reshape(k // 512, 16, n))


def unpack_weight(words, scales, fmt):
    g, p, n, _ = words.shape
    if fmt == "e4m3":
        vals = np.ascontiguousarray(words).view(ml_dtypes.float8_e4m3fn).astype(np.float64)
    else:
        nib = np.empty((g, p, n, 4), np.uint8)
        nib[..., 0::2] = words & 0xF
        nib[..., 1::2] = words >> 4
        vals = E2M1[nib]
    vals = vals * np.repeat(np.exp2(scales.astype(np.float64) - 127.0), 8, axis=1)[..., None]
    return vals.transpose(0, 1, 3, 2).reshape(g * 512, n)

def pack4(w):
    words, scales = pack_weight(w, "e2m1")
    return words.reshape(words.shape[0], 128, -1), scales


def unpack4(words, scales):
    return unpack_weight(words.reshape(words.shape[0], 128, -1, 2), scales, "e2m1")


def kspread(k):
    return np.exp2(np.repeat(np.random.randint(-6, 7, k // 32), 32).astype(np.float64))


B, T, C, NH, NKV, HS = 2, 1536, 2048, 16, 4, 128
EPS = 1e-6
ROPE_THETA = 10000.0
HALF = HS // 2
KW = NKV * HS


def rmsnorm(u, gain):
    ms = np.mean(np.square(u), axis=-1, keepdims=True)
    return u * (1.0 / np.sqrt(ms + EPS)) * gain


def rope_cos_sin():
    inv_freq = ROPE_THETA ** (-np.arange(0, HS, 2, dtype=np.float64) / HS)
    ang = np.arange(T, dtype=np.float64)[:, None] * inv_freq[None, :]
    return np.cos(ang), np.sin(ang)


def apply_rope(u, cos, sin):
    u1, u2 = u[..., :HALF], u[..., HALF:]
    c = cos[None, :, None, :]
    s = sin[None, :, None, :]
    return np.concatenate([u1 * c - u2 * s, u1 * s + u2 * c], axis=-1)


def setup_inputs():
    s = kspread(C)
    x = np.random.standard_normal((B, T, C)) * s
    x_words, x_scales = pack4(x.reshape(B * T, C).T)
    Wq_words, Wq_scales = pack4(np.random.standard_normal((C, NH * HS)) / np.sqrt(C) / s[:, None])
    Wkv_words, Wkv_scales = pack4(np.random.standard_normal((C, 2 * KW)) / np.sqrt(C) / s[:, None])
    return {
        "x_words": x_words,
        "x_scales": x_scales,
        "Wq_words": Wq_words,
        "Wq_scales": Wq_scales,
        "Wkv_words": Wkv_words,
        "Wkv_scales": Wkv_scales,
        "q_scale": bf(1.0 + 0.1 * np.random.standard_normal(HS)),
        "k_scale": bf(1.0 + 0.1 * np.random.standard_normal(HS)),
        "v1": bf(np.random.standard_normal((B, T, NKV, HS))),
        "value_lambda": bf(np.random.uniform(0.2, 0.7, (1,))),
    }


def reference(x_words, x_scales, Wq_words, Wq_scales, Wkv_words, Wkv_scales, q_scale, k_scale, v1, value_lambda):
    xq = unpack4(x_words, x_scales).T.reshape(B, T, C)
    q = (xq @ unpack4(Wq_words, Wq_scales)).reshape(B, T, NH, HS)
    kv = xq @ unpack4(Wkv_words, Wkv_scales)
    k = kv[..., :KW].reshape(B, T, NKV, HS)
    v = kv[..., KW:].reshape(B, T, NKV, HS)
    lam = f64(value_lambda).reshape(())
    v = v + (1.0 - lam) * f64(v1)
    q = rmsnorm(q, f64(q_scale))
    k = rmsnorm(k, f64(k_scale))
    cos, sin = rope_cos_sin()
    return apply_rope(q, cos, sin), apply_rope(k, cos, sin), v

@@ -1,0 +1,373 @@
+import math
+from contextlib import ExitStack
+
+import concourse.mybir as mybir
+
+F32 = mybir.dt.float32
+BF16 = mybir.dt.bfloat16
+I32 = mybir.dt.int32
+U8 = mybir.dt.uint8
+FP4X4 = mybir.dt.float4_e2m1fn_x4
+ACT = mybir.ActivationFunctionType
+ALU = mybir.AluOpType
+
+P = 128
+TOKENS = 3072
+POSITIONS = 1536
+C_IN = 2048
+HEAD = 128
+HALF = 64
+Q_HEADS = 16
+KV_HEADS = 4
+PASSES = C_IN // 512
+N_TILE = 512
+HEADS_PER_BANK = N_TILE // HEAD
+Q_BANKS = Q_HEADS * HEAD // N_TILE
+K_BANK = Q_BANKS
+V_BANK = Q_BANKS + 1
+ROPE_BANKS = Q_BANKS + 1
+ROPE_HEADS = ROPE_BANKS * HEADS_PER_BANK
+ROPE_COLS = ROPE_BANKS * N_TILE
+TOKEN_TILES = TOKENS // P
+POS_TILES = POSITIONS // P
+CHUNK_TILES = 4
+CHUNKS = TOKEN_TILES // CHUNK_TILES
+EPS = 1e-6
+ROPE_THETA = 10000.0
+
+LAG = 3
+FUSED_LAST = 2
+HOLD_V = 3
+VECTOR_TABLES = 1
+FIRST_ANGLES = 4
+HEAD_TABLES = 8
+LATE_TABLES = {1: (8, 10), 3: (10, 12)}
+PROD_C_BUFS = 5
+ACC_BUFS = 7
+TAIL_GROUPS = {TOKEN_TILES - 2: ((0, 3), (3, 5)), TOKEN_TILES - 1: ((0, 2), (2, 4), (4, 5))}
+
+FLOPS = 2 * TOKENS * C_IN * (Q_HEADS + 2 * KV_HEADS) * HEAD
+
+
+def tile_attention_pa_kernel(
+    tc, x_words, x_scales, Wq_words, Wq_scales, Wkv_words, Wkv_scales,
+    q_scale, k_scale, v1, value_lambda, out_0, out_1, out_2,
+):
+    nc = tc.nc
+    q_out = out_0.rearrange("b t h d -> (b t) (h d)")
+    k_out = out_1.rearrange("b t h d -> (b t) (h d)")
+    v_out = out_2.rearrange("b t h d -> (b t) (h d)")
+    v1_rows = v1.rearrange("b t h d -> (b t) (h d)")
+
+    with ExitStack() as ctx:
+        keep = ctx.enter_context(tc.tile_pool(name="keep", bufs=1))
+        work = ctx.enter_context(tc.tile_pool(name="work", bufs=1))
+        psum = ctx.enter_context(tc.psum_pool(name="psum", bufs=1))
+        ctx.enter_context(
+            tc.manual_schedule(
+                engines={mybir.EngineType.PE, mybir.EngineType.Activation, mybir.EngineType.DVE, mybir.EngineType.Pool}
+            )
+        )
+
+        x_codes = []
+        v1_tiles = []
+        for c in range(CHUNKS):
+            xc = keep.tile([P, PASSES, 2 * CHUNK_TILES * P], U8, name="x_codes%d" % c, align_bytes=64)
+            vt = keep.tile([P, CHUNK_TILES, N_TILE], BF16, name="v1_tile%d" % c)
+            x_codes.append(xc)
+            v1_tiles.append(vt)
+        x_planes = []
+        for i in range(2):
+            xp = keep.tile([P, PASSES, CHUNK_TILES * P], U8, name="x_planes%d" % i, align_bytes=64)
+            x_planes.append(xp)
+        w_codes = []
+        for n in range(V_BANK + 1):
+            wc = keep.tile([P, PASSES, 2 * N_TILE], U8, name="w_codes%d" % n, align_bytes=64)
+            w_codes.append(wc)
+        w_planes_a = keep.tile([P, PASSES, N_TILE], U8, name="w_planes_a", align_bytes=64)
+        w_planes_b = keep.tile([P, PASSES, 3 * N_TILE], U8, name="w_planes_b", align_bytes=64)
+        w_planes_c = keep.tile([P, PASSES, 2 * N_TILE], U8, name="w_planes_c", align_bytes=64)
+
+        def w_plane(n, g):
+            if n == 0:
+                return w_planes_a[:, g, :]
+            if n < Q_BANKS:
+                return w_planes_b[:, g, (n - 1) * N_TILE : n * N_TILE]
+            return w_planes_c[:, g, (n - Q_BANKS) * N_TILE : (n - Q_BANKS + 1) * N_TILE]
+
+        def load_codes(dst, words, first_byte, n_bytes):
+            nc.sync.dma_start(
+                out=dst[:].bitcast(I32),
+                in_=words[:, :, first_byte : first_byte + n_bytes].rearrange("g p n -> p g n").bitcast(I32),
+            )
+
+        def load_planes(dst, scales, first_col, n_cols):
+            for quad in range(4):
+                nc.sync.dma_start(
+                    out=dst[32 * quad : 32 * quad + 4, :, :].bitcast(I32),
+                    in_=scales[:, 4 * quad : 4 * quad + 4, first_col : first_col + n_cols]
+                    .rearrange("g r n -> r g n")
+                    .bitcast(I32),
+                )
+
+        def load_x_planes(c):
+            load_planes(x_planes[c % 2], x_scales, c * CHUNK_TILES * P, CHUNK_TILES * P)
+
+        def load_x_codes(c):
+            load_codes(x_codes[c], x_words, 2 * c * CHUNK_TILES * P, 2 * CHUNK_TILES * P)
+
+        def load_w_codes(n):
+            if n < Q_BANKS:
+                load_codes(w_codes[n], Wq_words, 2 * n * N_TILE, 2 * N_TILE)
+            else:
+                load_codes(w_codes[n], Wkv_words, 2 * (n - Q_BANKS) * N_TILE, 2 * N_TILE)
+
+        def load_v1(c):
+            nc.sync.dma_start(
+                out=v1_tiles[c][:],
+                in_=v1_rows[c * CHUNK_TILES * P : (c + 1) * CHUNK_TILES * P, :].rearrange("(t p) d -> p t d", p=P),
+            )
+
+        gain_row = keep.tile([P, N_TILE], BF16, name="gain_row")
+        pos_i = keep.tile([P, POS_TILES], I32, name="pos_i")
+        zero_col = keep.tile([P, 1], F32, name="zero_col")
+        warm = keep.tile([P, 1], F32, name="warm")
+        ones = keep.tile([P, P], BF16, name="ones")
+
+        load_x_codes(0)
+        load_w_codes(0)
+        nc.vector.memset(x_planes[0][:].bitcast(I32), 0)
+        nc.vector.memset(w_planes_a[:].bitcast(I32), 0)
+        load_x_planes(0)
+        load_planes(w_planes_a, Wq_scales, 0, N_TILE)
+        nc.vector.memset(gain_row[:], 0.0)
+        nc.vector.memset(zero_col[:], 0.0)
+        nc.scalar.activation(out=warm[:], in_=zero_col[:], func=ACT.Sin)
+
+        nc.gpsimd.iota(pos_i[:], pattern=[[P, POS_TILES]], base=0, channel_multiplier=1)
+        nc.gpsimd.dma_start(out=gain_row[0:1, 0:HEAD], in_=q_scale.unsqueeze(0))
+        nc.gpsimd.dma_start(out=gain_row[0:1, HEAD : 2 * HEAD], in_=k_scale.unsqueeze(0))
+        nc.gpsimd.dma_start(out=gain_row[0:1, 2 * HEAD : 2 * HEAD + 1], in_=value_lambda.unsqueeze(0))
+
+        nc.vector.memset(w_planes_b[:].bitcast(I32), 0)
+        load_planes(w_planes_b, Wq_scales, N_TILE, 3 * N_TILE)
+        for n in range(1, Q_BANKS):
+            load_w_codes(n)
+
+        freq = keep.tile([P, HALF], F32, name="freq")
+        nc.vector.memset(freq[:], 1.0)
+        nc.vector.tensor_scalar(out=freq[:], in0=freq[:], scalar1=1.0 / (2.0 * math.pi), scalar2=None, op0=ALU.mult)
+        ratio = ROPE_THETA ** (-2.0 / HEAD)
+        for bit in range(6):
+            run = 1 << bit
+            odd = freq[:].rearrange("p (a two b) -> p a two b", two=2, b=run)[:, :, 1, :]
+            nc.vector.tensor_scalar(out=odd, in0=odd, scalar1=ratio ** run, scalar2=None, op0=ALU.mult)
+        half_pi = keep.tile([P, 1], F32, name="half_pi")
+        nc.vector.tensor_scalar(out=half_pi[:], in0=zero_col[:], scalar1=math.pi / 2.0, scalar2=None, op0=ALU.add)
+        pos_f = keep.tile([P, POS_TILES], F32, name="pos_f")
+        nc.vector.tensor_copy(out=pos_f[:], in_=pos_i[:])
+
+        turns = keep.tile([P, POS_TILES, HALF], F32, name="turns")
+        whole = keep.tile([P, POS_TILES, HALF], I32, name="whole")
+        cos_t = keep.tile([P, POS_TILES, HALF], F32, name="cos_t")
+        sin_t = keep.tile([P, POS_TILES, HALF], F32, name="sin_t")
+        gains = keep.tile([P, 2 * HEAD], F32, name="gains")
+        gains_pm = keep.tile([P, 2 * HEAD], F32, name="gains_pm")
+        one_minus_lambda = keep.tile([P, 1], F32, name="one_minus_lambda")
+        tab_cos = keep.tile([P, POS_TILES, 2 * HEAD], F32, name="tab_cos")
+        tab_sin = keep.tile([P, POS_TILES, 2 * HEAD], F32, name="tab_sin")
+
+        def angles(j0, j1):
+            nj = j1 - j0
+            tj = turns[:, j0:j1, :]
+            nc.vector.tensor_tensor(
+                out=tj,
+                in0=pos_f[:, j0:j1].unsqueeze(2).to_broadcast([P, nj, HALF]),
+                in1=freq[:].unsqueeze(1).to_broadcast([P, nj, HALF]),
+                op=ALU.mult,
+            )
+            nc.vector.tensor_copy(out=whole[:, j0:j1, :], in_=tj)
+            nc.vector.tensor_tensor(out=tj, in0=tj, in1=whole[:, j0:j1, :], op=ALU.subtract)
+            nc.scalar.activation(out=sin_t[:, j0:j1, :], in_=tj, func=ACT.Sin, scale=2.0 * math.pi)
+            nc.scalar.activation(out=tj, in_=tj, func=ACT.Abs)
+            nc.scalar.activation(out=cos_t[:, j0:j1, :], in_=tj, func=ACT.Sin, scale=-2.0 * math.pi, bias=half_pi[:, 0:1])
+
+        def build_tables(eng, j0, j1):
+            nj = j1 - j0
+            for tab, gain, trig in ((tab_cos, gains, cos_t), (tab_sin, gains_pm, sin_t)):
+                eng.tensor_tensor(
+                    out=tab[:, j0:j1, :].rearrange("p j (r i) -> p j r i", i=HALF),
+                    in0=gain[:].rearrange("p (r i) -> p r i", i=HALF).unsqueeze(1).to_broadcast([P, nj, 4, HALF]),
+                    in1=trig[:, j0:j1, :].unsqueeze(2).to_broadcast([P, nj, 4, HALF]),
+                    op=ALU.mult,
+                )
+
+        angles(0, FIRST_ANGLES)
+        nc.vector.memset(ones[:], 1.0)
+        nc.vector.memset(w_planes_c[:].bitcast(I32), 0)
+        load_planes(w_planes_c, Wkv_scales, 0, 2 * N_TILE)
+        load_w_codes(K_BANK)
+        load_w_codes(V_BANK)
+        load_v1(0)
+        angles(FIRST_ANGLES, POS_TILES)
+        nc.vector.memset(x_planes[1][:].bitcast(I32), 0)
+
+        gain_ps = psum.tile([P, N_TILE], F32, name="gain_ps")
+        nc.tensor.matmul(out=gain_ps[:], lhsT=ones[:], rhs=gain_row[:], start=True, stop=True)
+        nc.scalar.copy(out=gains[:], in_=gain_ps[:, 0 : 2 * HEAD])
+        gp = gain_ps[:, 0 : 2 * HEAD].rearrange("p (w s i) -> p w s i", s=2, i=HALF)
+        gm = gains_pm[:].rearrange("p (w s i) -> p w s i", s=2, i=HALF)
+        nc.scalar.copy(out=gm[:, :, 0, :], in_=gp[:, :, 0, :])
+        nc.scalar.activation(out=gm[:, :, 1, :], in_=gp[:, :, 1, :], func=ACT.Copy, scale=-1.0)
+        nc.scalar.activation(
+            out=one_minus_lambda[:], in_=gain_ps[:, 2 * HEAD : 2 * HEAD + 1], func=ACT.Copy, scale=-1.0, bias=1.0
+        )
+        warm2 = keep.tile([P, 1], F32, name="warm2")
+        nc.scalar.activation(
+            out=warm2[:], in_=cos_t[:, POS_TILES - 1, HALF - 1 : HALF], func=ACT.Abs_reciprocal_sqrt, scale=1.0, bias=2.0
+        )
+        build_tables(nc.vector, 0, VECTOR_TABLES)
+        build_tables(nc.gpsimd, VECTOR_TABLES, 2)
+        for j0 in range(2, HEAD_TABLES, 2):
+            build_tables(nc.gpsimd, j0, j0 + 2)
+
+        prod_c = {}
+        prod_s = {}
+        sumsq = {}
+        rstd = {}
+
+        def fused(t, n):
+            return n == K_BANK or t >= TOKEN_TILES - FUSED_LAST
+
+        def project(t, n):
+            c = t // CHUNK_TILES
+            r = t % CHUNK_TILES
+            acc = psum.tile([P, N_TILE], F32, name="acc", bufs=ACC_BUFS)
+            for g in range(PASSES):
+                nc.tensor.matmul_mx(
+                    out=acc[:],
+                    lhsT=x_codes[c][:, g, 2 * r * P : 2 * (r + 1) * P].bitcast(FP4X4),
+                    lhsT_scale=x_planes[c % 2][:, g, r * P : (r + 1) * P],
+                    rhs=w_codes[n][:, g, :].bitcast(FP4X4),
+                    rhs_scale=w_plane(n, g),
+                    start=(g == 0),
+                    stop=(g == PASSES - 1),
+                )
+            return acc
+
+        def squares(t, n, acc):
+            for h in range(HEADS_PER_BANK):
+                junk = work.tile([P, HEAD], BF16, name="junk", bufs=4)
+                col = n * HEADS_PER_BANK + h
+                nc.scalar.activation(
+                    out=junk[:], in_=acc[:, h * HEAD : (h + 1) * HEAD], func=ACT.Square,
+                    accum_out=sumsq[t][:, col : col + 1],
+                )
+
+        def inv_norm(t, n0, n1):
+            cols = slice(n0 * HEADS_PER_BANK, n1 * HEADS_PER_BANK)
+            nc.scalar.activation(
+                out=rstd[t][:, cols], in_=sumsq[t][:, cols], func=ACT.Abs_reciprocal_sqrt, scale=1.0 / HEAD, bias=EPS
+            )
+
+        def products(t, n, acc):
+            j = t % POS_TILES
+            which = 0 if n < Q_BANKS else 1
+            for tab, prod in ((tab_cos, prod_c[t]), (tab_sin, prod_s[t])):
+                table = tab[:, j, which * HEAD : (which + 1) * HEAD]
+                if fused(t, n):
+                    for h in range(HEADS_PER_BANK):
+                        col = n * HEADS_PER_BANK + h
+                        nc.vector.scalar_tensor_tensor(
+                            out=prod[:, col * HEAD : (col + 1) * HEAD], in0=acc[:, h * HEAD : (h + 1) * HEAD],
+                            scalar=rstd[t][:, col : col + 1], in1=table, op0=ALU.mult, op1=ALU.mult,
+                        )
+                else:
+                    nc.vector.tensor_tensor(
+                        out=prod[:, n * N_TILE : (n + 1) * N_TILE].rearrange("p (h d) -> p h d", d=HEAD),
+                        in0=acc[:].rearrange("p (h d) -> p h d", d=HEAD),
+                        in1=table.unsqueeze(1).to_broadcast([P, HEADS_PER_BANK, HEAD]),
+                        op=ALU.mult,
+                    )
+
+        def add_halves(eng, t, n0, n1):
+            cols = slice(n0 * N_TILE, n1 * N_TILE)
+            pc = prod_c[t][:, cols].rearrange("p (h s i) -> p h s i", s=2, i=HALF)
+            ps = prod_s[t][:, cols].rearrange("p (h s i) -> p h s i", s=2, i=HALF)
+            for s in range(2):
+                eng.tensor_tensor(out=pc[:, :, s, :], in0=pc[:, :, s, :], in1=ps[:, :, 1 - s, :], op=ALU.add)
+
+        def store(t, n):
+            rows = slice(t * P, (t + 1) * P)
+            cols = slice(n * N_TILE, (n + 1) * N_TILE)
+            if n < Q_BANKS:
+                nc.sync.dma_start(out=q_out[rows, cols], in_=prod_c[t][:, cols])
+            else:
+                nc.sync.dma_start(out=k_out[rows, :], in_=prod_c[t][:, cols])
+
+        def finish(t, n):
+            for h in range(n * HEADS_PER_BANK, (n + 1) * HEADS_PER_BANK):
+                nc.scalar.activation(
+                    out=prod_c[t][:, h * HEAD : (h + 1) * HEAD], in_=prod_c[t][:, h * HEAD : (h + 1) * HEAD],
+                    func=ACT.Copy, scale=rstd[t][:, h : h + 1],
+                )
+            store(t, n)
+
+        def values(t):
+            c = t // CHUNK_TILES
+            r = t % CHUNK_TILES
+            acc = project(t, V_BANK)
+            v_new = work.tile([P, N_TILE], F32, name="v_new", bufs=4)
+            nc.vector.scalar_tensor_tensor(
+                out=v_new[:], in0=v1_tiles[c][:, r, :], scalar=one_minus_lambda[:, 0:1], in1=acc[:],
+                op0=ALU.mult, op1=ALU.add,
+            )
+            nc.sync.dma_start(out=v_out[t * P : (t + 1) * P, :], in_=v_new[:])
+
+        def groups(t):
+            return TAIL_GROUPS.get(t, ((0, ROPE_BANKS),))
+
+        due = []
+        served = 0
+        for t in range(TOKEN_TILES):
+            if t % CHUNK_TILES == 0 and t // CHUNK_TILES + 1 < CHUNKS:
+                c = t // CHUNK_TILES + 1
+                load_x_planes(c)
+                load_x_codes(c)
+                load_v1(c)
+            prod_c[t] = work.tile([P, ROPE_COLS], F32, name="prod_c", bufs=PROD_C_BUFS)
+            prod_s[t] = work.tile([P, ROPE_COLS], F32, name="prod_s", bufs=3)
+            sumsq[t] = work.tile([P, ROPE_HEADS], F32, name="sumsq", bufs=5)
+            rstd[t] = work.tile([P, ROPE_HEADS], F32, name="rstd", bufs=5)
+            if t >= LAG:
+                due.extend([(t - LAG, n) for n in range(ROPE_BANKS) if not fused(t - LAG, n)])
+            for n in range(ROPE_BANKS):
+                acc = project(t, n)
+                squares(t, n, acc)
+                if fused(t, n):
+                    inv_norm(t, n, n + 1)
+                elif n == Q_BANKS - 1:
+                    inv_norm(t, 0, Q_BANKS)
+                products(t, n, acc)
+                for n0, n1 in groups(t):
+                    if n == n1 - 1:
+                        add_halves(nc.gpsimd, t, n0, n1)
+                        for nn in range(n0, n1):
+                            if fused(t, nn):
+                                store(t, nn)
+                if n >= 1 and served < len(due):
+                    finish(*due[served])
+                    served += 1
+            if t in LATE_TABLES:
+                build_tables(nc.gpsimd, *LATE_TABLES[t])
+            if t < TOKEN_TILES - HOLD_V:
+                values(t)
+            while served < len(due):
+                finish(*due[served])
+                served += 1
+        for t in range(TOKEN_TILES - HOLD_V, TOKEN_TILES):
+            values(t)
+        for t in range(TOKEN_TILES - LAG, TOKEN_TILES):
+            for n in range(ROPE_BANKS):
+                if not fused(t, n):
+                    finish(t, n)

@@ -35,16 +35,20 @@ CHUNKS = TOKEN_TILES // CHUNK_TILES
 EPS = 1e-6
 ROPE_THETA = 10000.0
 
-LAG = 3
-FUSED_LAST = 2
-HOLD_V = 3
-VECTOR_TABLES = 1
-FIRST_ANGLES = 4
-HEAD_TABLES = 8
-LATE_TABLES = {1: (8, 10), 3: (10, 12)}
+DELAY = 8
+EARLY_DELAY = 14
+EARLY_TILES = 5
+TAIL_DELAY = 4
 PROD_C_BUFS = 5
 ACC_BUFS = 7
-TAIL_GROUPS = {TOKEN_TILES - 2: ((0, 3), (3, 5)), TOKEN_TILES - 1: ((0, 2), (2, 4), (4, 5))}
+FIRST_BLOCK = 2
+HOLD_V = 4
+VECTOR_TABLES = 1
+FIRST_ANGLES = 4
+WARM_MATMULS = 12
+BODY_GROUPS = ((0, 3), (3, 5))
+TAIL_GROUPS = {TOKEN_TILES - 2: ((0, 2), (2, 4), (4, 5)), TOKEN_TILES - 1: ((0, 1), (1, 2), (2, 3), (3, 4), (4, 5))}
+VECTOR_ADDS = ()
 
 FLOPS = 2 * TOKENS * C_IN * (Q_HEADS + 2 * KV_HEADS) * HEAD
 
@@ -63,11 +67,7 @@ def tile_attention_pa_kernel(
         keep = ctx.enter_context(tc.tile_pool(name="keep", bufs=1))
         work = ctx.enter_context(tc.tile_pool(name="work", bufs=1))
         psum = ctx.enter_context(tc.psum_pool(name="psum", bufs=1))
-        ctx.enter_context(
-            tc.manual_schedule(
-                engines={mybir.EngineType.PE, mybir.EngineType.Activation, mybir.EngineType.DVE, mybir.EngineType.Pool}
-            )
-        )
+        ctx.enter_context(tc.manual_schedule())
 
         x_codes = []
         v1_tiles = []
@@ -129,6 +129,7 @@ def tile_attention_pa_kernel(
             )
 
         gain_row = keep.tile([P, N_TILE], BF16, name="gain_row")
+        zero_row = keep.tile([P, N_TILE], BF16, name="zero_row")
         pos_i = keep.tile([P, POS_TILES], I32, name="pos_i")
         zero_col = keep.tile([P, 1], F32, name="zero_col")
         warm = keep.tile([P, 1], F32, name="warm")
@@ -138,21 +139,39 @@ def tile_attention_pa_kernel(
         load_w_codes(0)
         nc.vector.memset(x_planes[0][:].bitcast(I32), 0)
         nc.vector.memset(w_planes_a[:].bitcast(I32), 0)
+        nc.vector.memset(gain_row[:], 0.0)
         load_x_planes(0)
         load_planes(w_planes_a, Wq_scales, 0, N_TILE)
-        nc.vector.memset(gain_row[:], 0.0)
+        nc.sync.dma_start(out=gain_row[0:1, 0:HEAD], in_=q_scale.unsqueeze(0))
+        nc.sync.dma_start(out=gain_row[0:1, HEAD : 2 * HEAD], in_=k_scale.unsqueeze(0))
         nc.vector.memset(zero_col[:], 0.0)
         nc.scalar.activation(out=warm[:], in_=zero_col[:], func=ACT.Sin)
 
         nc.gpsimd.iota(pos_i[:], pattern=[[P, POS_TILES]], base=0, channel_multiplier=1)
-        nc.gpsimd.dma_start(out=gain_row[0:1, 0:HEAD], in_=q_scale.unsqueeze(0))
-        nc.gpsimd.dma_start(out=gain_row[0:1, HEAD : 2 * HEAD], in_=k_scale.unsqueeze(0))
-        nc.gpsimd.dma_start(out=gain_row[0:1, 2 * HEAD : 2 * HEAD + 1], in_=value_lambda.unsqueeze(0))
+        nc.gpsimd.memset(ones[:], 1.0)
+        nc.gpsimd.memset(zero_row[:], 0.0)
+        nc.gpsimd.memset(w_planes_c[:].bitcast(F32), 0.0)
+        nc.gpsimd.memset(x_planes[1][:].bitcast(F32), 0.0)
 
         nc.vector.memset(w_planes_b[:].bitcast(I32), 0)
         load_planes(w_planes_b, Wq_scales, N_TILE, 3 * N_TILE)
         for n in range(1, Q_BANKS):
             load_w_codes(n)
+        nc.sync.dma_start(out=gain_row[0:1, 2 * HEAD : 2 * HEAD + 1], in_=value_lambda.unsqueeze(0))
+        load_planes(w_planes_c, Wkv_scales, 0, 2 * N_TILE)
+        load_w_codes(K_BANK)
+        load_w_codes(V_BANK)
+        load_v1(0)
+
+        warm_ps = psum.tile([P, N_TILE], F32, name="acc", bufs=ACC_BUFS)
+        gain_ps = psum.tile([P, N_TILE], F32, name="gain_ps")
+
+        def warm_up():
+            for i in range(WARM_MATMULS):
+                nc.tensor.matmul(out=warm_ps[:], lhsT=ones[:], rhs=zero_row[:], start=True, stop=True)
+
+        warm_up()
+        nc.tensor.matmul(out=gain_ps[:, 0 : 2 * HEAD], lhsT=ones[:], rhs=gain_row[:, 0 : 2 * HEAD], start=True, stop=True)
 
         freq = keep.tile([P, HALF], F32, name="freq")
         nc.vector.memset(freq[:], 1.0)
@@ -203,32 +222,15 @@ def tile_attention_pa_kernel(
                 )
 
         angles(0, FIRST_ANGLES)
-        nc.vector.memset(ones[:], 1.0)
-        nc.vector.memset(w_planes_c[:].bitcast(I32), 0)
-        load_planes(w_planes_c, Wkv_scales, 0, 2 * N_TILE)
-        load_w_codes(K_BANK)
-        load_w_codes(V_BANK)
-        load_v1(0)
         angles(FIRST_ANGLES, POS_TILES)
-        nc.vector.memset(x_planes[1][:].bitcast(I32), 0)
-
-        gain_ps = psum.tile([P, N_TILE], F32, name="gain_ps")
-        nc.tensor.matmul(out=gain_ps[:], lhsT=ones[:], rhs=gain_row[:], start=True, stop=True)
         nc.scalar.copy(out=gains[:], in_=gain_ps[:, 0 : 2 * HEAD])
         gp = gain_ps[:, 0 : 2 * HEAD].rearrange("p (w s i) -> p w s i", s=2, i=HALF)
         gm = gains_pm[:].rearrange("p (w s i) -> p w s i", s=2, i=HALF)
         nc.scalar.copy(out=gm[:, :, 0, :], in_=gp[:, :, 0, :])
         nc.scalar.activation(out=gm[:, :, 1, :], in_=gp[:, :, 1, :], func=ACT.Copy, scale=-1.0)
-        nc.scalar.activation(
-            out=one_minus_lambda[:], in_=gain_ps[:, 2 * HEAD : 2 * HEAD + 1], func=ACT.Copy, scale=-1.0, bias=1.0
-        )
-        warm2 = keep.tile([P, 1], F32, name="warm2")
-        nc.scalar.activation(
-            out=warm2[:], in_=cos_t[:, POS_TILES - 1, HALF - 1 : HALF], func=ACT.Abs_reciprocal_sqrt, scale=1.0, bias=2.0
-        )
         build_tables(nc.vector, 0, VECTOR_TABLES)
         build_tables(nc.gpsimd, VECTOR_TABLES, 2)
-        for j0 in range(2, HEAD_TABLES, 2):
+        for j0 in range(2, POS_TILES, 2):
             build_tables(nc.gpsimd, j0, j0 + 2)
 
         prod_c = {}
@@ -237,7 +239,7 @@ def tile_attention_pa_kernel(
         rstd = {}
 
         def fused(t, n):
-            return n == K_BANK or t >= TOKEN_TILES - FUSED_LAST
+            return n == K_BANK
 
         def project(t, n):
             c = t // CHUNK_TILES
@@ -294,8 +296,7 @@ def tile_attention_pa_kernel(
             cols = slice(n0 * N_TILE, n1 * N_TILE)
             pc = prod_c[t][:, cols].rearrange("p (h s i) -> p h s i", s=2, i=HALF)
             ps = prod_s[t][:, cols].rearrange("p (h s i) -> p h s i", s=2, i=HALF)
-            for s in range(2):
-                eng.tensor_tensor(out=pc[:, :, s, :], in0=pc[:, :, s, :], in1=ps[:, :, 1 - s, :], op=ALU.add)
+            eng.tensor_tensor(out=pc, in0=pc, in1=ps[:, :, ::-1, :], op=ALU.add)
 
         def store(t, n):
             rows = slice(t * P, (t + 1) * P)
@@ -306,11 +307,12 @@ def tile_attention_pa_kernel(
                 nc.sync.dma_start(out=k_out[rows, :], in_=prod_c[t][:, cols])
 
         def finish(t, n):
-            for h in range(n * HEADS_PER_BANK, (n + 1) * HEADS_PER_BANK):
-                nc.scalar.activation(
-                    out=prod_c[t][:, h * HEAD : (h + 1) * HEAD], in_=prod_c[t][:, h * HEAD : (h + 1) * HEAD],
-                    func=ACT.Copy, scale=rstd[t][:, h : h + 1],
-                )
+            if not fused(t, n):
+                for h in range(n * HEADS_PER_BANK, (n + 1) * HEADS_PER_BANK):
+                    nc.scalar.activation(
+                        out=prod_c[t][:, h * HEAD : (h + 1) * HEAD], in_=prod_c[t][:, h * HEAD : (h + 1) * HEAD],
+                        func=ACT.Copy, scale=rstd[t][:, h : h + 1],
+                    )
             store(t, n)
 
         def values(t):
@@ -324,50 +326,60 @@ def tile_attention_pa_kernel(
             )
             nc.sync.dma_start(out=v_out[t * P : (t + 1) * P, :], in_=v_new[:])
 
-        def groups(t):
-            return TAIL_GROUPS.get(t, ((0, ROPE_BANKS),))
+        def lambda_column():
+            nc.tensor.matmul(
+                out=gain_ps[:, 2 * HEAD : 4 * HEAD], lhsT=ones[:], rhs=gain_row[:, 2 * HEAD : 4 * HEAD], start=True, stop=True
+            )
+            nc.scalar.activation(
+                out=one_minus_lambda[:], in_=gain_ps[:, 2 * HEAD : 2 * HEAD + 1], func=ACT.Copy, scale=-1.0, bias=1.0
+            )
+
+        steps = []
+        for n in range(V_BANK + 1):
+            for t in range(FIRST_BLOCK):
+                steps.append((t, n))
+        for t in range(FIRST_BLOCK, TOKEN_TILES):
+            for n in range(V_BANK + 1):
+                if n < V_BANK or t < TOKEN_TILES - HOLD_V:
+                    steps.append((t, n))
+                if t == TOKEN_TILES - 1 and 1 <= n < V_BANK:
+                    steps.append((TOKEN_TILES - HOLD_V + n - 1, V_BANK))
 
         due = []
         served = 0
-        for t in range(TOKEN_TILES):
-            if t % CHUNK_TILES == 0 and t // CHUNK_TILES + 1 < CHUNKS:
-                c = t // CHUNK_TILES + 1
-                load_x_planes(c)
-                load_x_codes(c)
-                load_v1(c)
-            prod_c[t] = work.tile([P, ROPE_COLS], F32, name="prod_c", bufs=PROD_C_BUFS)
-            prod_s[t] = work.tile([P, ROPE_COLS], F32, name="prod_s", bufs=3)
-            sumsq[t] = work.tile([P, ROPE_HEADS], F32, name="sumsq", bufs=5)
-            rstd[t] = work.tile([P, ROPE_HEADS], F32, name="rstd", bufs=5)
-            if t >= LAG:
-                due.extend([(t - LAG, n) for n in range(ROPE_BANKS) if not fused(t - LAG, n)])
-            for n in range(ROPE_BANKS):
-                acc = project(t, n)
-                squares(t, n, acc)
-                if fused(t, n):
-                    inv_norm(t, n, n + 1)
-                elif n == Q_BANKS - 1:
-                    inv_norm(t, 0, Q_BANKS)
-                products(t, n, acc)
-                for n0, n1 in groups(t):
-                    if n == n1 - 1:
-                        add_halves(nc.gpsimd, t, n0, n1)
-                        for nn in range(n0, n1):
-                            if fused(t, nn):
-                                store(t, nn)
-                if n >= 1 and served < len(due):
-                    finish(*due[served])
-                    served += 1
-            if t in LATE_TABLES:
-                build_tables(nc.gpsimd, *LATE_TABLES[t])
-            if t < TOKEN_TILES - HOLD_V:
+        for i, (t, n) in enumerate(steps):
+            last_tile = t == TOKEN_TILES - 1 or (n == V_BANK and t >= TOKEN_TILES - HOLD_V)
+            if n == 0:
+                if t % CHUNK_TILES == 0 and t // CHUNK_TILES + 1 < CHUNKS:
+                    c = t // CHUNK_TILES + 1
+                    load_x_planes(c)
+                    load_x_codes(c)
+                    load_v1(c)
+                prod_c[t] = work.tile([P, ROPE_COLS], F32, name="prod_c", bufs=PROD_C_BUFS)
+                prod_s[t] = work.tile([P, ROPE_COLS], F32, name="prod_s", bufs=3)
+                sumsq[t] = work.tile([P, ROPE_HEADS], F32, name="sumsq", bufs=PROD_C_BUFS + 1)
+                rstd[t] = work.tile([P, ROPE_HEADS], F32, name="rstd", bufs=PROD_C_BUFS + 1)
+            if n == V_BANK:
                 values(t)
-            while served < len(due):
-                finish(*due[served])
-                served += 1
-        for t in range(TOKEN_TILES - HOLD_V, TOKEN_TILES):
-            values(t)
-        for t in range(TOKEN_TILES - LAG, TOKEN_TILES):
-            for n in range(ROPE_BANKS):
-                if not fused(t, n):
-                    finish(t, n)
+            else:
+                acc = project(t, n)
+                if (t, n) == (0, 1):
+                    lambda_column()
+                squares(t, n, acc)
+                if fused(t, n) or t >= TOKEN_TILES - 2:
+                    inv_norm(t, n, n + 1)
+                products(t, n, acc)
+                for n0, n1 in TAIL_GROUPS.get(t, BODY_GROUPS):
+                    if n == n1 - 1:
+                        add_halves(nc.vector if (t, n0) in VECTOR_ADDS else nc.gpsimd, t, n0, n1)
+                        wait_steps = TAIL_DELAY if t >= TOKEN_TILES - 2 else (EARLY_DELAY if t < EARLY_TILES else DELAY)
+                        due.extend([(i + wait_steps, t, nn) for nn in range(n0, n1)])
+            for k in range(2 if last_tile else 1):
+                if served < len(due) and due[served][0] <= i:
+                    finish(due[served][1], due[served][2])
+                    served += 1
+            if n == Q_BANKS - 1 and t < TOKEN_TILES - 2:
+                inv_norm(t, 0, Q_BANKS)
+        while served < len(due):
+            finish(due[served][1], due[served][2])
+            served += 1

@@ -35,11 +35,12 @@ CHUNKS = TOKEN_TILES // CHUNK_TILES
 EPS = 1e-6
 ROPE_THETA = 10000.0
 
-DELAY = 8
-EARLY_DELAY = 14
+SCALE_DELAY = 8
+STORE_DELAY = 4
+EARLY_EXTRA = 6
 EARLY_TILES = 5
-TAIL_DELAY = 4
-PROD_C_BUFS = 5
+PROD_BUFS = 4
+FIRST_FUSED = 2
 ACC_BUFS = 7
 FIRST_BLOCK = 2
 HOLD_V = 4
@@ -193,8 +194,7 @@ def tile_attention_pa_kernel(
         gains = keep.tile([P, 2 * HEAD], F32, name="gains")
         gains_pm = keep.tile([P, 2 * HEAD], F32, name="gains_pm")
         one_minus_lambda = keep.tile([P, 1], F32, name="one_minus_lambda")
-        tab_cos = keep.tile([P, POS_TILES, 2 * HEAD], F32, name="tab_cos")
-        tab_sin = keep.tile([P, POS_TILES, 2 * HEAD], F32, name="tab_sin")
+        tables = keep.tile([P, POS_TILES, 2, 2 * HEAD], F32, name="tables")
 
         def angles(j0, j1):
             nj = j1 - j0
@@ -213,9 +213,9 @@ def tile_attention_pa_kernel(
 
         def build_tables(eng, j0, j1):
             nj = j1 - j0
-            for tab, gain, trig in ((tab_cos, gains, cos_t), (tab_sin, gains_pm, sin_t)):
+            for kind, gain, trig in ((0, gains, cos_t), (1, gains_pm, sin_t)):
                 eng.tensor_tensor(
-                    out=tab[:, j0:j1, :].rearrange("p j (r i) -> p j r i", i=HALF),
+                    out=tables[:, j0:j1, kind, :].rearrange("p j (r i) -> p j r i", i=HALF),
                     in0=gain[:].rearrange("p (r i) -> p r i", i=HALF).unsqueeze(1).to_broadcast([P, nj, 4, HALF]),
                     in1=trig[:, j0:j1, :].unsqueeze(2).to_broadcast([P, nj, 4, HALF]),
                     op=ALU.mult,
@@ -233,13 +233,12 @@ def tile_attention_pa_kernel(
         for j0 in range(2, POS_TILES, 2):
             build_tables(nc.gpsimd, j0, j0 + 2)
 
-        prod_c = {}
-        prod_s = {}
+        prod = {}
         sumsq = {}
         rstd = {}
 
         def fused(t, n):
-            return n == K_BANK
+            return n >= FIRST_FUSED or t >= TOKEN_TILES - 2
 
         def project(t, n):
             c = t // CHUNK_TILES
@@ -275,50 +274,49 @@ def tile_attention_pa_kernel(
         def products(t, n, acc):
             j = t % POS_TILES
             which = 0 if n < Q_BANKS else 1
-            for tab, prod in ((tab_cos, prod_c[t]), (tab_sin, prod_s[t])):
-                table = tab[:, j, which * HEAD : (which + 1) * HEAD]
-                if fused(t, n):
-                    for h in range(HEADS_PER_BANK):
-                        col = n * HEADS_PER_BANK + h
-                        nc.vector.scalar_tensor_tensor(
-                            out=prod[:, col * HEAD : (col + 1) * HEAD], in0=acc[:, h * HEAD : (h + 1) * HEAD],
-                            scalar=rstd[t][:, col : col + 1], in1=table, op0=ALU.mult, op1=ALU.mult,
-                        )
-                else:
-                    nc.vector.tensor_tensor(
-                        out=prod[:, n * N_TILE : (n + 1) * N_TILE].rearrange("p (h d) -> p h d", d=HEAD),
-                        in0=acc[:].rearrange("p (h d) -> p h d", d=HEAD),
-                        in1=table.unsqueeze(1).to_broadcast([P, HEADS_PER_BANK, HEAD]),
-                        op=ALU.mult,
+            table = tables[:, j, :, which * HEAD : (which + 1) * HEAD]
+            if fused(t, n):
+                for h in range(HEADS_PER_BANK):
+                    col = n * HEADS_PER_BANK + h
+                    nc.vector.scalar_tensor_tensor(
+                        out=prod[t][:, :, col * HEAD : (col + 1) * HEAD],
+                        in0=acc[:, h * HEAD : (h + 1) * HEAD].unsqueeze(1).to_broadcast([P, 2, HEAD]),
+                        scalar=rstd[t][:, col : col + 1], in1=table, op0=ALU.mult, op1=ALU.mult,
                     )
+            else:
+                nc.vector.tensor_tensor(
+                    out=prod[t][:, :, n * N_TILE : (n + 1) * N_TILE].rearrange("p s (h d) -> p s h d", d=HEAD),
+                    in0=acc[:].rearrange("p (h d) -> p h d", d=HEAD).unsqueeze(1).to_broadcast([P, 2, HEADS_PER_BANK, HEAD]),
+                    in1=table.unsqueeze(2).to_broadcast([P, 2, HEADS_PER_BANK, HEAD]),
+                    op=ALU.mult,
+                )
 
         def add_halves(eng, t, n0, n1):
             cols = slice(n0 * N_TILE, n1 * N_TILE)
-            pc = prod_c[t][:, cols].rearrange("p (h s i) -> p h s i", s=2, i=HALF)
-            ps = prod_s[t][:, cols].rearrange("p (h s i) -> p h s i", s=2, i=HALF)
+            pc = prod[t][:, 0, cols].rearrange("p (h s i) -> p h s i", s=2, i=HALF)
+            ps = prod[t][:, 1, cols].rearrange("p (h s i) -> p h s i", s=2, i=HALF)
             eng.tensor_tensor(out=pc, in0=pc, in1=ps[:, :, ::-1, :], op=ALU.add)
 
         def store(t, n):
             rows = slice(t * P, (t + 1) * P)
             cols = slice(n * N_TILE, (n + 1) * N_TILE)
             if n < Q_BANKS:
-                nc.sync.dma_start(out=q_out[rows, cols], in_=prod_c[t][:, cols])
+                nc.sync.dma_start(out=q_out[rows, cols], in_=prod[t][:, 0, cols])
             else:
-                nc.sync.dma_start(out=k_out[rows, :], in_=prod_c[t][:, cols])
+                nc.sync.dma_start(out=k_out[rows, :], in_=prod[t][:, 0, cols])
 
         def finish(t, n):
             if not fused(t, n):
                 for h in range(n * HEADS_PER_BANK, (n + 1) * HEADS_PER_BANK):
                     nc.scalar.activation(
-                        out=prod_c[t][:, h * HEAD : (h + 1) * HEAD], in_=prod_c[t][:, h * HEAD : (h + 1) * HEAD],
+                        out=prod[t][:, 0, h * HEAD : (h + 1) * HEAD], in_=prod[t][:, 0, h * HEAD : (h + 1) * HEAD],
                         func=ACT.Copy, scale=rstd[t][:, h : h + 1],
                     )
             store(t, n)
 
-        def values(t):
+        def values(t, acc):
             c = t // CHUNK_TILES
             r = t % CHUNK_TILES
-            acc = project(t, V_BANK)
             v_new = work.tile([P, N_TILE], F32, name="v_new", bufs=4)
             nc.vector.scalar_tensor_tensor(
                 out=v_new[:], in0=v1_tiles[c][:, r, :], scalar=one_minus_lambda[:, 0:1], in1=acc[:],
@@ -345,41 +343,59 @@ def tile_attention_pa_kernel(
                 if t == TOKEN_TILES - 1 and 1 <= n < V_BANK:
                     steps.append((TOKEN_TILES - HOLD_V + n - 1, V_BANK))
 
-        due = []
-        served = 0
-        for i, (t, n) in enumerate(steps):
-            last_tile = t == TOKEN_TILES - 1 or (n == V_BANK and t >= TOKEN_TILES - HOLD_V)
-            if n == 0:
-                if t % CHUNK_TILES == 0 and t // CHUNK_TILES + 1 < CHUNKS:
-                    c = t // CHUNK_TILES + 1
-                    load_x_planes(c)
-                    load_x_codes(c)
-                    load_v1(c)
-                prod_c[t] = work.tile([P, ROPE_COLS], F32, name="prod_c", bufs=PROD_C_BUFS)
-                prod_s[t] = work.tile([P, ROPE_COLS], F32, name="prod_s", bufs=3)
-                sumsq[t] = work.tile([P, ROPE_HEADS], F32, name="sumsq", bufs=PROD_C_BUFS + 1)
-                rstd[t] = work.tile([P, ROPE_HEADS], F32, name="rstd", bufs=PROD_C_BUFS + 1)
-            if n == V_BANK:
-                values(t)
-            else:
-                acc = project(t, n)
+        to_scale = []
+        to_store = []
+        scaled = 0
+        stored = 0
+        banks = {}
+        for i in range(len(steps) + 1):
+            if i < len(steps):
+                t, n = steps[i]
+                if n == 0:
+                    if t % CHUNK_TILES == 0 and t // CHUNK_TILES + 1 < CHUNKS:
+                        c = t // CHUNK_TILES + 1
+                        load_x_planes(c)
+                        load_x_codes(c)
+                        load_v1(c)
+                    prod[t] = work.tile([P, 2, ROPE_COLS], F32, name="prod", bufs=PROD_BUFS)
+                    sumsq[t] = work.tile([P, ROPE_HEADS], F32, name="sumsq", bufs=PROD_BUFS + 1)
+                    rstd[t] = work.tile([P, ROPE_HEADS], F32, name="rstd", bufs=PROD_BUFS + 1)
+                banks[i] = project(t, n)
                 if (t, n) == (0, 1):
                     lambda_column()
-                squares(t, n, acc)
-                if fused(t, n) or t >= TOKEN_TILES - 2:
+                if n < V_BANK:
+                    squares(t, n, banks[i])
+            if i == 0:
+                continue
+            t, n = steps[i - 1]
+            last_tile = t == TOKEN_TILES - 1 or (n == V_BANK and t >= TOKEN_TILES - HOLD_V)
+            if n == V_BANK:
+                values(t, banks[i - 1])
+            else:
+                if fused(t, n):
                     inv_norm(t, n, n + 1)
-                products(t, n, acc)
+                elif n == FIRST_FUSED - 1:
+                    inv_norm(t, 0, FIRST_FUSED)
+                products(t, n, banks[i - 1])
                 for n0, n1 in TAIL_GROUPS.get(t, BODY_GROUPS):
                     if n == n1 - 1:
                         add_halves(nc.vector if (t, n0) in VECTOR_ADDS else nc.gpsimd, t, n0, n1)
-                        wait_steps = TAIL_DELAY if t >= TOKEN_TILES - 2 else (EARLY_DELAY if t < EARLY_TILES else DELAY)
-                        due.extend([(i + wait_steps, t, nn) for nn in range(n0, n1)])
-            for k in range(2 if last_tile else 1):
-                if served < len(due) and due[served][0] <= i:
-                    finish(due[served][1], due[served][2])
-                    served += 1
-            if n == Q_BANKS - 1 and t < TOKEN_TILES - 2:
-                inv_norm(t, 0, Q_BANKS)
-        while served < len(due):
-            finish(due[served][1], due[served][2])
-            served += 1
+                        early = EARLY_EXTRA if t < EARLY_TILES else 0
+                        for nn in range(n0, n1):
+                            if fused(t, nn):
+                                to_store.append((i + STORE_DELAY + early, t, nn))
+                            else:
+                                to_scale.append((i + SCALE_DELAY + early, t, nn))
+            if scaled < len(to_scale) and to_scale[scaled][0] <= i:
+                finish(to_scale[scaled][1], to_scale[scaled][2])
+                scaled += 1
+            for k in range(2):
+                if stored < len(to_store) and to_store[stored][0] <= i:
+                    finish(to_store[stored][1], to_store[stored][2])
+                    stored += 1
+        while scaled < len(to_scale):
+            finish(to_scale[scaled][1], to_scale[scaled][2])
+            scaled += 1
+        while stored < len(to_store):
+            finish(to_store[stored][1], to_store[stored][2])
+            stored += 1

@@ -42,13 +42,14 @@ EARLY_TILES = 5
 PROD_BUFS = 4
 FIRST_FUSED = 2
 ACC_BUFS = 7
-FIRST_BLOCK = 2
-HOLD_V = 4
+FIRST_BLOCK = 3
+TAIL_V_AFTER = (1, 2, 3, 4)
+HOLD_V = len(TAIL_V_AFTER)
 VECTOR_TABLES = 1
 FIRST_ANGLES = 4
 WARM_MATMULS = 12
 BODY_GROUPS = ((0, 3), (3, 5))
-TAIL_GROUPS = {TOKEN_TILES - 2: ((0, 2), (2, 4), (4, 5)), TOKEN_TILES - 1: ((0, 1), (1, 2), (2, 3), (3, 4), (4, 5))}
+TAIL_GROUPS = {TOKEN_TILES - 1: ((0, 2), (2, 3), (3, 4), (4, 5))}
 VECTOR_ADDS = ()
 
 FLOPS = 2 * TOKENS * C_IN * (Q_HEADS + 2 * KV_HEADS) * HEAD
@@ -223,11 +224,15 @@ def tile_attention_pa_kernel(
 
         angles(0, FIRST_ANGLES)
         angles(FIRST_ANGLES, POS_TILES)
-        nc.scalar.copy(out=gains[:], in_=gain_ps[:, 0 : 2 * HEAD])
+        warm2 = keep.tile([P, 1], F32, name="warm2")
+        nc.scalar.activation(
+            out=warm2[:], in_=cos_t[:, POS_TILES - 1, HALF - 1 : HALF], func=ACT.Abs_reciprocal_sqrt, scale=1.0, bias=2.0
+        )
+        nc.vector.tensor_copy(out=gains[:], in_=gain_ps[:, 0 : 2 * HEAD])
         gp = gain_ps[:, 0 : 2 * HEAD].rearrange("p (w s i) -> p w s i", s=2, i=HALF)
         gm = gains_pm[:].rearrange("p (w s i) -> p w s i", s=2, i=HALF)
-        nc.scalar.copy(out=gm[:, :, 0, :], in_=gp[:, :, 0, :])
-        nc.scalar.activation(out=gm[:, :, 1, :], in_=gp[:, :, 1, :], func=ACT.Copy, scale=-1.0)
+        nc.vector.tensor_copy(out=gm[:, :, 0, :], in_=gp[:, :, 0, :])
+        nc.vector.tensor_scalar(out=gm[:, :, 1, :], in0=gp[:, :, 1, :], scalar1=-1.0, scalar2=None, op0=ALU.mult)
         build_tables(nc.vector, 0, VECTOR_TABLES)
         build_tables(nc.gpsimd, VECTOR_TABLES, 2)
         for j0 in range(2, POS_TILES, 2):
@@ -333,6 +338,7 @@ def tile_attention_pa_kernel(
             )
 
         steps = []
+        held = 0
         for n in range(V_BANK + 1):
             for t in range(FIRST_BLOCK):
                 steps.append((t, n))
@@ -340,8 +346,11 @@ def tile_attention_pa_kernel(
             for n in range(V_BANK + 1):
                 if n < V_BANK or t < TOKEN_TILES - HOLD_V:
                     steps.append((t, n))
-                if t == TOKEN_TILES - 1 and 1 <= n < V_BANK:
-                    steps.append((TOKEN_TILES - HOLD_V + n - 1, V_BANK))
+                if t == TOKEN_TILES - 1:
+                    for after in TAIL_V_AFTER:
+                        if after == n:
+                            steps.append((TOKEN_TILES - HOLD_V + held, V_BANK))
+                            held += 1
 
         to_scale = []
         to_store = []

@@ -103,8 +103,8 @@ def tile_attention_pa_kernel(
                 in_=words[:, :, first_byte : first_byte + n_bytes].rearrange("g p n -> p g n").bitcast(I32),
             )
 
-        def load_planes(dst, scales, first_col, n_cols):
-            for quad in range(4):
+        def load_planes(dst, scales, first_col, n_cols, quads=(0, 1, 2, 3)):
+            for quad in quads:
                 nc.sync.dma_start(
                     out=dst[32 * quad : 32 * quad + 4, :, :].bitcast(I32),
                     in_=scales[:, 4 * quad : 4 * quad + 4, first_col : first_col + n_cols]
@@ -137,13 +137,14 @@ def tile_attention_pa_kernel(
         warm = keep.tile([P, 1], F32, name="warm")
         ones = keep.tile([P, P], BF16, name="ones")
 
-        load_x_codes(0)
-        load_w_codes(0)
         nc.vector.memset(x_planes[0][:].bitcast(I32), 0)
         nc.vector.memset(w_planes_a[:].bitcast(I32), 0)
         nc.vector.memset(gain_row[:], 0.0)
         load_x_planes(0)
-        load_planes(w_planes_a, Wq_scales, 0, N_TILE)
+        load_planes(w_planes_a, Wq_scales, 0, N_TILE, (0, 1))
+        load_x_codes(0)
+        load_w_codes(0)
+        load_planes(w_planes_a, Wq_scales, 0, N_TILE, (2, 3))
         nc.sync.dma_start(out=gain_row[0:1, 0:HEAD], in_=q_scale.unsqueeze(0))
         nc.sync.dma_start(out=gain_row[0:1, HEAD : 2 * HEAD], in_=k_scale.unsqueeze(0))
         nc.vector.memset(zero_col[:], 0.0)
@@ -173,7 +174,6 @@ def tile_attention_pa_kernel(
                 nc.tensor.matmul(out=warm_ps[:], lhsT=ones[:], rhs=zero_row[:], start=True, stop=True)
 
         warm_up()
-        nc.tensor.matmul(out=gain_ps[:, 0 : 2 * HEAD], lhsT=ones[:], rhs=gain_row[:, 0 : 2 * HEAD], start=True, stop=True)
 
         freq = keep.tile([P, HALF], F32, name="freq")
         nc.vector.memset(freq[:], 1.0)
@@ -228,15 +228,17 @@ def tile_attention_pa_kernel(
         nc.scalar.activation(
             out=warm2[:], in_=cos_t[:, POS_TILES - 1, HALF - 1 : HALF], func=ACT.Abs_reciprocal_sqrt, scale=1.0, bias=2.0
         )
-        nc.vector.tensor_copy(out=gains[:], in_=gain_ps[:, 0 : 2 * HEAD])
-        gp = gain_ps[:, 0 : 2 * HEAD].rearrange("p (w s i) -> p w s i", s=2, i=HALF)
-        gm = gains_pm[:].rearrange("p (w s i) -> p w s i", s=2, i=HALF)
-        nc.vector.tensor_copy(out=gm[:, :, 0, :], in_=gp[:, :, 0, :])
-        nc.vector.tensor_scalar(out=gm[:, :, 1, :], in0=gp[:, :, 1, :], scalar1=-1.0, scalar2=None, op0=ALU.mult)
-        build_tables(nc.vector, 0, VECTOR_TABLES)
-        build_tables(nc.gpsimd, VECTOR_TABLES, 2)
-        for j0 in range(2, POS_TILES, 2):
-            build_tables(nc.gpsimd, j0, j0 + 2)
+        def gains_and_tables():
+            nc.tensor.matmul(out=gain_ps[:, 0 : 2 * HEAD], lhsT=ones[:], rhs=gain_row[:, 0 : 2 * HEAD], start=True, stop=True)
+            nc.vector.tensor_copy(out=gains[:], in_=gain_ps[:, 0 : 2 * HEAD])
+            gp = gain_ps[:, 0 : 2 * HEAD].rearrange("p (w s i) -> p w s i", s=2, i=HALF)
+            gm = gains_pm[:].rearrange("p (w s i) -> p w s i", s=2, i=HALF)
+            nc.vector.tensor_copy(out=gm[:, :, 0, :], in_=gp[:, :, 0, :])
+            nc.vector.tensor_scalar(out=gm[:, :, 1, :], in0=gp[:, :, 1, :], scalar1=-1.0, scalar2=None, op0=ALU.mult)
+            build_tables(nc.vector, 0, VECTOR_TABLES)
+            build_tables(nc.gpsimd, VECTOR_TABLES, 2)
+            for j0 in range(2, POS_TILES, 2):
+                build_tables(nc.gpsimd, j0, j0 + 2)
 
         prod = {}
         sumsq = {}
@@ -370,6 +372,8 @@ def tile_attention_pa_kernel(
                     sumsq[t] = work.tile([P, ROPE_HEADS], F32, name="sumsq", bufs=PROD_BUFS + 1)
                     rstd[t] = work.tile([P, ROPE_HEADS], F32, name="rstd", bufs=PROD_BUFS + 1)
                 banks[i] = project(t, n)
+                if i == 0:
+                    gains_and_tables()
                 if (t, n) == (0, 1):
                     lambda_column()
                 if n < V_BANK:

@@ -43,7 +43,7 @@ PROD_BUFS = 4
 FIRST_FUSED = 2
 ACC_BUFS = 7
 FIRST_BLOCK = 3
-TAIL_V_AFTER = (1, 2, 3, 4)
+TAIL_V_AFTER = (4, 4, 4, 4)
 HOLD_V = len(TAIL_V_AFTER)
 VECTOR_TABLES = 1
 FIRST_ANGLES = 4
@@ -324,7 +324,7 @@ def tile_attention_pa_kernel(
         def values(t, acc):
             c = t // CHUNK_TILES
             r = t % CHUNK_TILES
-            v_new = work.tile([P, N_TILE], F32, name="v_new", bufs=4)
+            v_new = work.tile([P, N_TILE], F32, name="v_new", bufs=6)
             nc.vector.scalar_tensor_tensor(
                 out=v_new[:], in0=v1_tiles[c][:, r, :], scalar=one_minus_lambda[:, 0:1], in1=acc[:],
                 op0=ALU.mult, op1=ALU.add,
@@ -374,7 +374,7 @@ def tile_attention_pa_kernel(
                 banks[i] = project(t, n)
                 if i == 0:
                     gains_and_tables()
-                if (t, n) == (0, 1):
+                if (t, n) == (0, 3):
                     lambda_column()
                 if n < V_BANK:
                     squares(t, n, banks[i])

@@ -43,8 +43,9 @@ PROD_BUFS = 4
 FIRST_FUSED = 2
 ACC_BUFS = 7
 FIRST_BLOCK = 3
-TAIL_V_AFTER = (4, 4, 4, 4)
-HOLD_V = len(TAIL_V_AFTER)
+HELD_V = (5, 8, 11, 14, 17, 20, 23)
+V_AFTER = {(23, 1): 1, (23, 2): 1, (23, 3): 1}
+X_PLANE_BUFS = 6
 VECTOR_TABLES = 1
 FIRST_ANGLES = 4
 WARM_MATMULS = 12
@@ -79,7 +80,7 @@ def tile_attention_pa_kernel(
             x_codes.append(xc)
             v1_tiles.append(vt)
         x_planes = []
-        for i in range(2):
+        for i in range(X_PLANE_BUFS):
             xp = keep.tile([P, PASSES, CHUNK_TILES * P], U8, name="x_planes%d" % i, align_bytes=64)
             x_planes.append(xp)
         w_codes = []
@@ -113,7 +114,7 @@ def tile_attention_pa_kernel(
                 )
 
         def load_x_planes(c):
-            load_planes(x_planes[c % 2], x_scales, c * CHUNK_TILES * P, CHUNK_TILES * P)
+            load_planes(x_planes[c], x_scales, c * CHUNK_TILES * P, CHUNK_TILES * P)
 
         def load_x_codes(c):
             load_codes(x_codes[c], x_words, 2 * c * CHUNK_TILES * P, 2 * CHUNK_TILES * P)
@@ -239,6 +240,8 @@ def tile_attention_pa_kernel(
             build_tables(nc.gpsimd, VECTOR_TABLES, 2)
             for j0 in range(2, POS_TILES, 2):
                 build_tables(nc.gpsimd, j0, j0 + 2)
+            for c in range(2, X_PLANE_BUFS):
+                nc.gpsimd.memset(x_planes[c][:].bitcast(F32), 0.0)
 
         prod = {}
         sumsq = {}
@@ -255,7 +258,7 @@ def tile_attention_pa_kernel(
                 nc.tensor.matmul_mx(
                     out=acc[:],
                     lhsT=x_codes[c][:, g, 2 * r * P : 2 * (r + 1) * P].bitcast(FP4X4),
-                    lhsT_scale=x_planes[c % 2][:, g, r * P : (r + 1) * P],
+                    lhsT_scale=x_planes[c][:, g, r * P : (r + 1) * P],
                     rhs=w_codes[n][:, g, :].bitcast(FP4X4),
                     rhs_scale=w_plane(n, g),
                     start=(g == 0),
@@ -340,19 +343,19 @@ def tile_attention_pa_kernel(
             )
 
         steps = []
-        held = 0
         for n in range(V_BANK + 1):
             for t in range(FIRST_BLOCK):
                 steps.append((t, n))
+        woven = 0
         for t in range(FIRST_BLOCK, TOKEN_TILES):
             for n in range(V_BANK + 1):
-                if n < V_BANK or t < TOKEN_TILES - HOLD_V:
+                if n < V_BANK or t not in HELD_V:
                     steps.append((t, n))
-                if t == TOKEN_TILES - 1:
-                    for after in TAIL_V_AFTER:
-                        if after == n:
-                            steps.append((TOKEN_TILES - HOLD_V + held, V_BANK))
-                            held += 1
+                for k in range(V_AFTER.get((t, n), 0)):
+                    steps.append((HELD_V[woven], V_BANK))
+                    woven += 1
+        for t in HELD_V[woven:]:
+            steps.append((t, V_BANK))
 
         to_scale = []
         to_store = []
@@ -381,7 +384,6 @@ def tile_attention_pa_kernel(
             if i == 0:
                 continue
             t, n = steps[i - 1]
-            last_tile = t == TOKEN_TILES - 1 or (n == V_BANK and t >= TOKEN_TILES - HOLD_V)
             if n == V_BANK:
                 values(t, banks[i - 1])
             else:

@@ -48,7 +48,7 @@ V_AFTER = {(23, 1): 1, (23, 2): 1, (23, 3): 1}
 X_PLANE_BUFS = 6
 VECTOR_TABLES = 1
 FIRST_ANGLES = 4
-WARM_MATMULS = 12
+WARM_MATMULS = 7
 BODY_GROUPS = ((0, 3), (3, 5))
 TAIL_GROUPS = {TOKEN_TILES - 1: ((0, 2), (2, 3), (3, 4), (4, 5))}
 VECTOR_ADDS = ()

@@ -324,7 +324,7 @@ def tile_attention_pa_kernel(
                     )
             store(t, n)
 
-        def values(t, acc):
+        def values(t, acc, queue):
             c = t // CHUNK_TILES
             r = t % CHUNK_TILES
             v_new = work.tile([P, N_TILE], F32, name="v_new", bufs=6)
@@ -332,7 +332,7 @@ def tile_attention_pa_kernel(
                 out=v_new[:], in0=v1_tiles[c][:, r, :], scalar=one_minus_lambda[:, 0:1], in1=acc[:],
                 op0=ALU.mult, op1=ALU.add,
             )
-            nc.sync.dma_start(out=v_out[t * P : (t + 1) * P, :], in_=v_new[:])
+            queue.dma_start(out=v_out[t * P : (t + 1) * P, :], in_=v_new[:])
 
         def lambda_column():
             nc.tensor.matmul(
@@ -385,7 +385,7 @@ def tile_attention_pa_kernel(
                 continue
             t, n = steps[i - 1]
             if n == V_BANK:
-                values(t, banks[i - 1])
+                values(t, banks[i - 1], nc.scalar if i - 1 >= len(steps) - len(HELD_V) + woven else nc.sync)
             else:
                 if fused(t, n):
                     inv_norm(t, n, n + 1)

@@ -37,12 +37,13 @@ ROPE_THETA = 10000.0
 
 SCALE_DELAY = 8
 STORE_DELAY = 4
-EARLY_EXTRA = 6
+EARLY_EXTRA = 2
 EARLY_TILES = 5
 PROD_BUFS = 4
 FIRST_FUSED = 2
 ACC_BUFS = 7
 FIRST_BLOCK = 3
+EARLY_V = 4
 HELD_V = (5, 8, 11, 14, 17, 20, 23)
 V_AFTER = {(23, 1): 1, (23, 2): 1, (23, 3): 1}
 X_PLANE_BUFS = 6
@@ -89,14 +90,17 @@ def tile_attention_pa_kernel(
             w_codes.append(wc)
         w_planes_a = keep.tile([P, PASSES, N_TILE], U8, name="w_planes_a", align_bytes=64)
         w_planes_b = keep.tile([P, PASSES, 3 * N_TILE], U8, name="w_planes_b", align_bytes=64)
-        w_planes_c = keep.tile([P, PASSES, 2 * N_TILE], U8, name="w_planes_c", align_bytes=64)
+        w_planes_k = keep.tile([P, PASSES, N_TILE], U8, name="w_planes_k", align_bytes=64)
+        w_planes_v = keep.tile([P, PASSES, N_TILE], U8, name="w_planes_v", align_bytes=64)
 
         def w_plane(n, g):
             if n == 0:
                 return w_planes_a[:, g, :]
             if n < Q_BANKS:
                 return w_planes_b[:, g, (n - 1) * N_TILE : n * N_TILE]
-            return w_planes_c[:, g, (n - Q_BANKS) * N_TILE : (n - Q_BANKS + 1) * N_TILE]
+            if n == K_BANK:
+                return w_planes_k[:, g, :]
+            return w_planes_v[:, g, :]
 
         def load_codes(dst, words, first_byte, n_bytes):
             nc.sync.dma_start(
@@ -139,13 +143,15 @@ def tile_attention_pa_kernel(
         ones = keep.tile([P, P], BF16, name="ones")
 
         nc.vector.memset(x_planes[0][:].bitcast(I32), 0)
-        nc.vector.memset(w_planes_a[:].bitcast(I32), 0)
+        nc.vector.memset(w_planes_v[:].bitcast(I32), 0)
         nc.vector.memset(gain_row[:], 0.0)
         load_x_planes(0)
-        load_planes(w_planes_a, Wq_scales, 0, N_TILE, (0, 1))
+        load_planes(w_planes_v, Wkv_scales, N_TILE, N_TILE, (0, 1))
         load_x_codes(0)
-        load_w_codes(0)
-        load_planes(w_planes_a, Wq_scales, 0, N_TILE, (2, 3))
+        load_w_codes(V_BANK)
+        load_planes(w_planes_v, Wkv_scales, N_TILE, N_TILE, (2, 3))
+        nc.sync.dma_start(out=gain_row[0:1, 2 * HEAD : 2 * HEAD + 1], in_=value_lambda.unsqueeze(0))
+        load_v1(0)
         nc.sync.dma_start(out=gain_row[0:1, 0:HEAD], in_=q_scale.unsqueeze(0))
         nc.sync.dma_start(out=gain_row[0:1, HEAD : 2 * HEAD], in_=k_scale.unsqueeze(0))
         nc.vector.memset(zero_col[:], 0.0)
@@ -154,18 +160,18 @@ def tile_attention_pa_kernel(
         nc.gpsimd.iota(pos_i[:], pattern=[[P, POS_TILES]], base=0, channel_multiplier=1)
         nc.gpsimd.memset(ones[:], 1.0)
         nc.gpsimd.memset(zero_row[:], 0.0)
-        nc.gpsimd.memset(w_planes_c[:].bitcast(F32), 0.0)
+        nc.gpsimd.memset(w_planes_k[:].bitcast(F32), 0.0)
         nc.gpsimd.memset(x_planes[1][:].bitcast(F32), 0.0)
 
+        nc.vector.memset(w_planes_a[:].bitcast(I32), 0)
+        load_planes(w_planes_a, Wq_scales, 0, N_TILE)
+        load_w_codes(0)
         nc.vector.memset(w_planes_b[:].bitcast(I32), 0)
         load_planes(w_planes_b, Wq_scales, N_TILE, 3 * N_TILE)
         for n in range(1, Q_BANKS):
             load_w_codes(n)
-        nc.sync.dma_start(out=gain_row[0:1, 2 * HEAD : 2 * HEAD + 1], in_=value_lambda.unsqueeze(0))
-        load_planes(w_planes_c, Wkv_scales, 0, 2 * N_TILE)
+        load_planes(w_planes_k, Wkv_scales, 0, N_TILE)
         load_w_codes(K_BANK)
-        load_w_codes(V_BANK)
-        load_v1(0)
 
         warm_ps = psum.tile([P, N_TILE], F32, name="acc", bufs=ACC_BUFS)
         gain_ps = psum.tile([P, N_TILE], F32, name="gain_ps")
@@ -338,18 +344,21 @@ def tile_attention_pa_kernel(
             nc.tensor.matmul(
                 out=gain_ps[:, 2 * HEAD : 4 * HEAD], lhsT=ones[:], rhs=gain_row[:, 2 * HEAD : 4 * HEAD], start=True, stop=True
             )
-            nc.scalar.activation(
-                out=one_minus_lambda[:], in_=gain_ps[:, 2 * HEAD : 2 * HEAD + 1], func=ACT.Copy, scale=-1.0, bias=1.0
+            nc.vector.tensor_scalar(
+                out=one_minus_lambda[:], in0=gain_ps[:, 2 * HEAD : 2 * HEAD + 1], scalar1=-1.0, scalar2=1.0,
+                op0=ALU.mult, op1=ALU.add,
             )
 
         steps = []
-        for n in range(V_BANK + 1):
+        for t in range(EARLY_V):
+            steps.append((t, V_BANK))
+        for n in range(V_BANK):
             for t in range(FIRST_BLOCK):
                 steps.append((t, n))
         woven = 0
         for t in range(FIRST_BLOCK, TOKEN_TILES):
             for n in range(V_BANK + 1):
-                if n < V_BANK or t not in HELD_V:
+                if n < V_BANK or (t not in HELD_V and t >= EARLY_V):
                     steps.append((t, n))
                 for k in range(V_AFTER.get((t, n), 0)):
                     steps.append((HELD_V[woven], V_BANK))
@@ -376,8 +385,6 @@ def tile_attention_pa_kernel(
                     rstd[t] = work.tile([P, ROPE_HEADS], F32, name="rstd", bufs=PROD_BUFS + 1)
                 banks[i] = project(t, n)
                 if i == 0:
-                    gains_and_tables()
-                if (t, n) == (0, 3):
                     lambda_column()
                 if n < V_BANK:
                     squares(t, n, banks[i])
@@ -408,6 +415,8 @@ def tile_attention_pa_kernel(
                 if stored < len(to_store) and to_store[stored][0] <= i:
                     finish(to_store[stored][1], to_store[stored][2])
                     stored += 1
+            if i == 1:
+                gains_and_tables()
         while scaled < len(to_scale):
             finish(to_scale[scaled][1], to_scale[scaled][2])
             scaled += 1

@@ -47,7 +47,7 @@ EARLY_V = 4
 HELD_V = (5, 8, 11, 14, 17, 20, 23)
 V_AFTER = {(23, 1): 1, (23, 2): 1, (23, 3): 1}
 X_PLANE_BUFS = 6
-VECTOR_TABLES = 1
+VECTOR_TABLES = 4
 FIRST_ANGLES = 4
 WARM_MATMULS = 7
 BODY_GROUPS = ((0, 3), (3, 5))
@@ -119,6 +119,9 @@ def tile_attention_pa_kernel(
 
         def load_x_planes(c):
             load_planes(x_planes[c], x_scales, c * CHUNK_TILES * P, CHUNK_TILES * P)
+
+        def fill_x_planes(c):
+            load_codes(x_planes[c], x_words, 0, CHUNK_TILES * P)
 
         def load_x_codes(c):
             load_codes(x_codes[c], x_words, 2 * c * CHUNK_TILES * P, 2 * CHUNK_TILES * P)
@@ -198,9 +201,8 @@ def tile_attention_pa_kernel(
         turns = keep.tile([P, POS_TILES, HALF], F32, name="turns")
         whole = keep.tile([P, POS_TILES, HALF], I32, name="whole")
         cos_t = keep.tile([P, POS_TILES, HALF], F32, name="cos_t")
-        sin_t = keep.tile([P, POS_TILES, HALF], F32, name="sin_t")
+        sin_pm = keep.tile([P, POS_TILES, 2, HALF], F32, name="sin_pm")
         gains = keep.tile([P, 2 * HEAD], F32, name="gains")
-        gains_pm = keep.tile([P, 2 * HEAD], F32, name="gains_pm")
         one_minus_lambda = keep.tile([P, 1], F32, name="one_minus_lambda")
         tables = keep.tile([P, POS_TILES, 2, 2 * HEAD], F32, name="tables")
 
@@ -215,19 +217,25 @@ def tile_attention_pa_kernel(
             )
             nc.vector.tensor_copy(out=whole[:, j0:j1, :], in_=tj)
             nc.vector.tensor_tensor(out=tj, in0=tj, in1=whole[:, j0:j1, :], op=ALU.subtract)
-            nc.scalar.activation(out=sin_t[:, j0:j1, :], in_=tj, func=ACT.Sin, scale=2.0 * math.pi)
+            nc.scalar.activation(out=sin_pm[:, j0:j1, 0, :], in_=tj, func=ACT.Sin, scale=2.0 * math.pi)
+            nc.scalar.activation(out=sin_pm[:, j0:j1, 1, :], in_=tj, func=ACT.Sin, scale=-2.0 * math.pi)
             nc.scalar.activation(out=tj, in_=tj, func=ACT.Abs)
             nc.scalar.activation(out=cos_t[:, j0:j1, :], in_=tj, func=ACT.Sin, scale=-2.0 * math.pi, bias=half_pi[:, 0:1])
 
-        def build_tables(eng, j0, j1):
+        def build_tables(eng, gain, j0, j1):
             nj = j1 - j0
-            for kind, gain, trig in ((0, gains, cos_t), (1, gains_pm, sin_t)):
-                eng.tensor_tensor(
-                    out=tables[:, j0:j1, kind, :].rearrange("p j (r i) -> p j r i", i=HALF),
-                    in0=gain[:].rearrange("p (r i) -> p r i", i=HALF).unsqueeze(1).to_broadcast([P, nj, 4, HALF]),
-                    in1=trig[:, j0:j1, :].unsqueeze(2).to_broadcast([P, nj, 4, HALF]),
-                    op=ALU.mult,
-                )
+            eng.tensor_tensor(
+                out=tables[:, j0:j1, 0, :].rearrange("p j (r i) -> p j r i", i=HALF),
+                in0=gain.rearrange("p (r i) -> p r i", i=HALF).unsqueeze(1).to_broadcast([P, nj, 4, HALF]),
+                in1=cos_t[:, j0:j1, :].unsqueeze(2).to_broadcast([P, nj, 4, HALF]),
+                op=ALU.mult,
+            )
+            eng.tensor_tensor(
+                out=tables[:, j0:j1, 1, :].rearrange("p j (w d) -> p j w d", d=HEAD),
+                in0=gain.rearrange("p (w d) -> p w d", d=HEAD).unsqueeze(1).to_broadcast([P, nj, 2, HEAD]),
+                in1=sin_pm[:, j0:j1, :, :].rearrange("p j s i -> p j (s i)").unsqueeze(2).to_broadcast([P, nj, 2, HEAD]),
+                op=ALU.mult,
+            )
 
         angles(0, FIRST_ANGLES)
         angles(FIRST_ANGLES, POS_TILES)
@@ -238,16 +246,9 @@ def tile_attention_pa_kernel(
         def gains_and_tables():
             nc.tensor.matmul(out=gain_ps[:, 0 : 2 * HEAD], lhsT=ones[:], rhs=gain_row[:, 0 : 2 * HEAD], start=True, stop=True)
             nc.vector.tensor_copy(out=gains[:], in_=gain_ps[:, 0 : 2 * HEAD])
-            gp = gain_ps[:, 0 : 2 * HEAD].rearrange("p (w s i) -> p w s i", s=2, i=HALF)
-            gm = gains_pm[:].rearrange("p (w s i) -> p w s i", s=2, i=HALF)
-            nc.vector.tensor_copy(out=gm[:, :, 0, :], in_=gp[:, :, 0, :])
-            nc.vector.tensor_scalar(out=gm[:, :, 1, :], in0=gp[:, :, 1, :], scalar1=-1.0, scalar2=None, op0=ALU.mult)
-            build_tables(nc.vector, 0, VECTOR_TABLES)
-            build_tables(nc.gpsimd, VECTOR_TABLES, 2)
-            for j0 in range(2, POS_TILES, 2):
-                build_tables(nc.gpsimd, j0, j0 + 2)
-            for c in range(2, X_PLANE_BUFS):
-                nc.gpsimd.memset(x_planes[c][:].bitcast(F32), 0.0)
+            build_tables(nc.vector, gain_ps[:, 0 : 2 * HEAD], 0, VECTOR_TABLES)
+            for j0 in range(VECTOR_TABLES, POS_TILES, 2):
+                build_tables(nc.gpsimd, gains[:], j0, j0 + 2)
 
         prod = {}
         sumsq = {}
@@ -380,6 +381,9 @@ def tile_attention_pa_kernel(
                         load_x_planes(c)
                         load_x_codes(c)
                         load_v1(c)
+                    if t == 0:
+                        for c in range(2, X_PLANE_BUFS):
+                            fill_x_planes(c)
                     prod[t] = work.tile([P, 2, ROPE_COLS], F32, name="prod", bufs=PROD_BUFS)
                     sumsq[t] = work.tile([P, ROPE_HEADS], F32, name="sumsq", bufs=PROD_BUFS + 1)
                     rstd[t] = work.tile([P, ROPE_HEADS], F32, name="rstd", bufs=PROD_BUFS + 1)

@@ -76,22 +76,22 @@ def tile_attention_pa_kernel(
         x_codes = []
         v1_tiles = []
         for c in range(CHUNKS):
-            xc = keep.tile([P, PASSES, 2 * CHUNK_TILES * P], U8, name="x_codes%d" % c, align_bytes=64)
-            vt = keep.tile([P, CHUNK_TILES, N_TILE], BF16, name="v1_tile%d" % c)
+            xc = keep.tile([P, PASSES, 2 * CHUNK_TILES * P], U8, name="x_codes%d" % c, align_bytes=256)
+            vt = keep.tile([P, CHUNK_TILES, N_TILE], BF16, name="v1_tile%d" % c, align_bytes=256)
             x_codes.append(xc)
             v1_tiles.append(vt)
         x_planes = []
         for i in range(X_PLANE_BUFS):
-            xp = keep.tile([P, PASSES, CHUNK_TILES * P], U8, name="x_planes%d" % i, align_bytes=64)
+            xp = keep.tile([P, PASSES, CHUNK_TILES * P], U8, name="x_planes%d" % i, align_bytes=256)
             x_planes.append(xp)
         w_codes = []
         for n in range(V_BANK + 1):
-            wc = keep.tile([P, PASSES, 2 * N_TILE], U8, name="w_codes%d" % n, align_bytes=64)
+            wc = keep.tile([P, PASSES, 2 * N_TILE], U8, name="w_codes%d" % n, align_bytes=256)
             w_codes.append(wc)
-        w_planes_a = keep.tile([P, PASSES, N_TILE], U8, name="w_planes_a", align_bytes=64)
-        w_planes_b = keep.tile([P, PASSES, 3 * N_TILE], U8, name="w_planes_b", align_bytes=64)
-        w_planes_k = keep.tile([P, PASSES, N_TILE], U8, name="w_planes_k", align_bytes=64)
-        w_planes_v = keep.tile([P, PASSES, N_TILE], U8, name="w_planes_v", align_bytes=64)
+        w_planes_a = keep.tile([P, PASSES, N_TILE], U8, name="w_planes_a", align_bytes=256)
+        w_planes_b = keep.tile([P, PASSES, 3 * N_TILE], U8, name="w_planes_b", align_bytes=256)
+        w_planes_k = keep.tile([P, PASSES, N_TILE], U8, name="w_planes_k", align_bytes=256)
+        w_planes_v = keep.tile([P, PASSES, N_TILE], U8, name="w_planes_v", align_bytes=256)
 
         def w_plane(n, g):
             if n == 0:
@@ -334,7 +334,7 @@ def tile_attention_pa_kernel(
         def values(t, acc, queue):
             c = t // CHUNK_TILES
             r = t % CHUNK_TILES
-            v_new = work.tile([P, N_TILE], F32, name="v_new", bufs=6)
+            v_new = work.tile([P, N_TILE], F32, name="v_new", bufs=6, align_bytes=256)
             nc.vector.scalar_tensor_tensor(
                 out=v_new[:], in0=v1_tiles[c][:, r, :], scalar=one_minus_lambda[:, 0:1], in1=acc[:],
                 op0=ALU.mult, op1=ALU.add,
@@ -384,7 +384,7 @@ def tile_attention_pa_kernel(
                     if t == 0:
                         for c in range(2, X_PLANE_BUFS):
                             fill_x_planes(c)
-                    prod[t] = work.tile([P, 2, ROPE_COLS], F32, name="prod", bufs=PROD_BUFS)
+                    prod[t] = work.tile([P, 2, ROPE_COLS], F32, name="prod", bufs=PROD_BUFS, align_bytes=256)
                     sumsq[t] = work.tile([P, ROPE_HEADS], F32, name="sumsq", bufs=PROD_BUFS + 1)
                     rstd[t] = work.tile([P, ROPE_HEADS], F32, name="rstd", bufs=PROD_BUFS + 1)
                 banks[i] = project(t, n)

import math
from contextlib import ExitStack

import concourse.mybir as mybir

F32 = mybir.dt.float32
BF16 = mybir.dt.bfloat16
I32 = mybir.dt.int32
U8 = mybir.dt.uint8
FP4X4 = mybir.dt.float4_e2m1fn_x4
ACT = mybir.ActivationFunctionType
ALU = mybir.AluOpType

P = 128
TOKENS = 3072
POSITIONS = 1536
C_IN = 2048
HEAD = 128
HALF = 64
Q_HEADS = 16
KV_HEADS = 4
PASSES = C_IN // 512
N_TILE = 512
HEADS_PER_BANK = N_TILE // HEAD
Q_BANKS = Q_HEADS * HEAD // N_TILE
K_BANK = Q_BANKS
V_BANK = Q_BANKS + 1
ROPE_BANKS = Q_BANKS + 1
ROPE_HEADS = ROPE_BANKS * HEADS_PER_BANK
ROPE_COLS = ROPE_BANKS * N_TILE
TOKEN_TILES = TOKENS // P
POS_TILES = POSITIONS // P
CHUNK_TILES = 4
CHUNKS = TOKEN_TILES // CHUNK_TILES
EPS = 1e-6
ROPE_THETA = 10000.0

SCALE_DELAY = 8
STORE_DELAY = 4
EARLY_EXTRA = 2
EARLY_TILES = 5
PROD_BUFS = 4
FIRST_FUSED = 2
ACC_BUFS = 7
FIRST_BLOCK = 3
EARLY_V = 4
HELD_V = (5, 8, 11, 14, 17, 20, 23)
V_AFTER = {(23, 1): 1, (23, 2): 1, (23, 3): 1}
X_PLANE_BUFS = 6
VECTOR_TABLES = 4
FIRST_ANGLES = 4
WARM_MATMULS = 7
BODY_GROUPS = ((0, 3), (3, 5))
TAIL_GROUPS = {TOKEN_TILES - 1: ((0, 2), (2, 3), (3, 4), (4, 5))}
VECTOR_ADDS = ()

FLOPS = 2 * TOKENS * C_IN * (Q_HEADS + 2 * KV_HEADS) * HEAD


def tile_attention_pa_kernel(
    tc, x_words, x_scales, Wq_words, Wq_scales, Wkv_words, Wkv_scales,
    q_scale, k_scale, v1, value_lambda, out_0, out_1, out_2,
):
    nc = tc.nc
    q_out = out_0.rearrange("b t h d -> (b t) (h d)")
    k_out = out_1.rearrange("b t h d -> (b t) (h d)")
    v_out = out_2.rearrange("b t h d -> (b t) (h d)")
    v1_rows = v1.rearrange("b t h d -> (b t) (h d)")

    with ExitStack() as ctx:
        keep = ctx.enter_context(tc.tile_pool(name="keep", bufs=1))
        work = ctx.enter_context(tc.tile_pool(name="work", bufs=1))
        psum = ctx.enter_context(tc.psum_pool(name="psum", bufs=1))
        ctx.enter_context(tc.manual_schedule())

        x_codes = []
        v1_tiles = []
        for c in range(CHUNKS):
            xc = keep.tile([P, PASSES, 2 * CHUNK_TILES * P], U8, name="x_codes%d" % c, align_bytes=256)
            vt = keep.tile([P, CHUNK_TILES, N_TILE], BF16, name="v1_tile%d" % c, align_bytes=256)
            x_codes.append(xc)
            v1_tiles.append(vt)
        x_planes = []
        for i in range(X_PLANE_BUFS):
            xp = keep.tile([P, PASSES, CHUNK_TILES * P], U8, name="x_planes%d" % i, align_bytes=256)
            x_planes.append(xp)
        w_codes = []
        for n in range(V_BANK + 1):
            wc = keep.tile([P, PASSES, 2 * N_TILE], U8, name="w_codes%d" % n, align_bytes=256)
            w_codes.append(wc)
        w_planes_a = keep.tile([P, PASSES, N_TILE], U8, name="w_planes_a", align_bytes=256)
        w_planes_b = keep.tile([P, PASSES, 3 * N_TILE], U8, name="w_planes_b", align_bytes=256)
        w_planes_k = keep.tile([P, PASSES, N_TILE], U8, name="w_planes_k", align_bytes=256)
        w_planes_v = keep.tile([P, PASSES, N_TILE], U8, name="w_planes_v", align_bytes=256)

        def w_plane(n, g):
            if n == 0:
                return w_planes_a[:, g, :]
            if n < Q_BANKS:
                return w_planes_b[:, g, (n - 1) * N_TILE : n * N_TILE]
            if n == K_BANK:
                return w_planes_k[:, g, :]
            return w_planes_v[:, g, :]

        def load_codes(dst, words, first_byte, n_bytes):
            nc.sync.dma_start(
                out=dst[:].bitcast(I32),
                in_=words[:, :, first_byte : first_byte + n_bytes].rearrange("g p n -> p g n").bitcast(I32),
            )

        def load_planes(dst, scales, first_col, n_cols, quads=(0, 1, 2, 3)):
            for quad in quads:
                nc.sync.dma_start(
                    out=dst[32 * quad : 32 * quad + 4, :, :].bitcast(I32),
                    in_=scales[:, 4 * quad : 4 * quad + 4, first_col : first_col + n_cols]
                    .rearrange("g r n -> r g n")
                    .bitcast(I32),
                )

        def load_x_planes(c):
            load_planes(x_planes[c], x_scales, c * CHUNK_TILES * P, CHUNK_TILES * P)

        def fill_x_planes(c):
            load_codes(x_planes[c], x_words, 0, CHUNK_TILES * P)

        def load_x_codes(c):
            load_codes(x_codes[c], x_words, 2 * c * CHUNK_TILES * P, 2 * CHUNK_TILES * P)

        def load_w_codes(n):
            if n < Q_BANKS:
                load_codes(w_codes[n], Wq_words, 2 * n * N_TILE, 2 * N_TILE)
            else:
                load_codes(w_codes[n], Wkv_words, 2 * (n - Q_BANKS) * N_TILE, 2 * N_TILE)

        def load_v1(c):
            nc.sync.dma_start(
                out=v1_tiles[c][:],
                in_=v1_rows[c * CHUNK_TILES * P : (c + 1) * CHUNK_TILES * P, :].rearrange("(t p) d -> p t d", p=P),
            )

        gain_row = keep.tile([P, N_TILE], BF16, name="gain_row")
        zero_row = keep.tile([P, N_TILE], BF16, name="zero_row")
        pos_i = keep.tile([P, POS_TILES], I32, name="pos_i")
        zero_col = keep.tile([P, 1], F32, name="zero_col")
        warm = keep.tile([P, 1], F32, name="warm")
        ones = keep.tile([P, P], BF16, name="ones")

        nc.vector.memset(x_planes[0][:].bitcast(I32), 0)
        nc.vector.memset(w_planes_v[:].bitcast(I32), 0)
        nc.vector.memset(gain_row[:], 0.0)
        load_x_planes(0)
        load_planes(w_planes_v, Wkv_scales, N_TILE, N_TILE, (0, 1))
        load_x_codes(0)
        load_w_codes(V_BANK)
        load_planes(w_planes_v, Wkv_scales, N_TILE, N_TILE, (2, 3))
        nc.sync.dma_start(out=gain_row[0:1, 2 * HEAD : 2 * HEAD + 1], in_=value_lambda.unsqueeze(0))
        load_v1(0)
        nc.sync.dma_start(out=gain_row[0:1, 0:HEAD], in_=q_scale.unsqueeze(0))
        nc.sync.dma_start(out=gain_row[0:1, HEAD : 2 * HEAD], in_=k_scale.unsqueeze(0))
        nc.vector.memset(zero_col[:], 0.0)
        nc.scalar.activation(out=warm[:], in_=zero_col[:], func=ACT.Sin)

        nc.gpsimd.iota(pos_i[:], pattern=[[P, POS_TILES]], base=0, channel_multiplier=1)
        nc.gpsimd.memset(ones[:], 1.0)
        nc.gpsimd.memset(zero_row[:], 0.0)
        nc.gpsimd.memset(w_planes_k[:].bitcast(F32), 0.0)
        nc.gpsimd.memset(x_planes[1][:].bitcast(F32), 0.0)

        nc.vector.memset(w_planes_a[:].bitcast(I32), 0)
        load_planes(w_planes_a, Wq_scales, 0, N_TILE)
        load_w_codes(0)
        nc.vector.memset(w_planes_b[:].bitcast(I32), 0)
        load_planes(w_planes_b, Wq_scales, N_TILE, 3 * N_TILE)
        for n in range(1, Q_BANKS):
            load_w_codes(n)
        load_planes(w_planes_k, Wkv_scales, 0, N_TILE)
        load_w_codes(K_BANK)

        warm_ps = psum.tile([P, N_TILE], F32, name="acc", bufs=ACC_BUFS)
        gain_ps = psum.tile([P, N_TILE], F32, name="gain_ps")

        def warm_up():
            for i in range(WARM_MATMULS):
                nc.tensor.matmul(out=warm_ps[:], lhsT=ones[:], rhs=zero_row[:], start=True, stop=True)

        warm_up()

        freq = keep.tile([P, HALF], F32, name="freq")
        nc.vector.memset(freq[:], 1.0)
        nc.vector.tensor_scalar(out=freq[:], in0=freq[:], scalar1=1.0 / (2.0 * math.pi), scalar2=None, op0=ALU.mult)
        ratio = ROPE_THETA ** (-2.0 / HEAD)
        for bit in range(6):
            run = 1 << bit
            odd = freq[:].rearrange("p (a two b) -> p a two b", two=2, b=run)[:, :, 1, :]
            nc.vector.tensor_scalar(out=odd, in0=odd, scalar1=ratio ** run, scalar2=None, op0=ALU.mult)
        half_pi = keep.tile([P, 1], F32, name="half_pi")
        nc.vector.tensor_scalar(out=half_pi[:], in0=zero_col[:], scalar1=math.pi / 2.0, scalar2=None, op0=ALU.add)
        pos_f = keep.tile([P, POS_TILES], F32, name="pos_f")
        nc.vector.tensor_copy(out=pos_f[:], in_=pos_i[:])

        turns = keep.tile([P, POS_TILES, HALF], F32, name="turns")
        whole = keep.tile([P, POS_TILES, HALF], I32, name="whole")
        cos_t = keep.tile([P, POS_TILES, HALF], F32, name="cos_t")
        sin_pm = keep.tile([P, POS_TILES, 2, HALF], F32, name="sin_pm")
        gains = keep.tile([P, 2 * HEAD], F32, name="gains")
        one_minus_lambda = keep.tile([P, 1], F32, name="one_minus_lambda")
        tables = keep.tile([P, POS_TILES, 2, 2 * HEAD], F32, name="tables")

        def angles(j0, j1):
            nj = j1 - j0
            tj = turns[:, j0:j1, :]
            nc.vector.tensor_tensor(
                out=tj,
                in0=pos_f[:, j0:j1].unsqueeze(2).to_broadcast([P, nj, HALF]),
                in1=freq[:].unsqueeze(1).to_broadcast([P, nj, HALF]),
                op=ALU.mult,
            )
            nc.vector.tensor_copy(out=whole[:, j0:j1, :], in_=tj)
            nc.vector.tensor_tensor(out=tj, in0=tj, in1=whole[:, j0:j1, :], op=ALU.subtract)
            nc.scalar.activation(out=sin_pm[:, j0:j1, 0, :], in_=tj, func=ACT.Sin, scale=2.0 * math.pi)
            nc.scalar.activation(out=sin_pm[:, j0:j1, 1, :], in_=tj, func=ACT.Sin, scale=-2.0 * math.pi)
            nc.scalar.activation(out=tj, in_=tj, func=ACT.Abs)
            nc.scalar.activation(out=cos_t[:, j0:j1, :], in_=tj, func=ACT.Sin, scale=-2.0 * math.pi, bias=half_pi[:, 0:1])

        def build_tables(eng, gain, j0, j1):
            nj = j1 - j0
            eng.tensor_tensor(
                out=tables[:, j0:j1, 0, :].rearrange("p j (r i) -> p j r i", i=HALF),
                in0=gain.rearrange("p (r i) -> p r i", i=HALF).unsqueeze(1).to_broadcast([P, nj, 4, HALF]),
                in1=cos_t[:, j0:j1, :].unsqueeze(2).to_broadcast([P, nj, 4, HALF]),
                op=ALU.mult,
            )
            eng.tensor_tensor(
                out=tables[:, j0:j1, 1, :].rearrange("p j (w d) -> p j w d", d=HEAD),
                in0=gain.rearrange("p (w d) -> p w d", d=HEAD).unsqueeze(1).to_broadcast([P, nj, 2, HEAD]),
                in1=sin_pm[:, j0:j1, :, :].rearrange("p j s i -> p j (s i)").unsqueeze(2).to_broadcast([P, nj, 2, HEAD]),
                op=ALU.mult,
            )

        angles(0, FIRST_ANGLES)
        angles(FIRST_ANGLES, POS_TILES)
        warm2 = keep.tile([P, 1], F32, name="warm2")
        nc.scalar.activation(
            out=warm2[:], in_=cos_t[:, POS_TILES - 1, HALF - 1 : HALF], func=ACT.Abs_reciprocal_sqrt, scale=1.0, bias=2.0
        )
        def gains_and_tables():
            nc.tensor.matmul(out=gain_ps[:, 0 : 2 * HEAD], lhsT=ones[:], rhs=gain_row[:, 0 : 2 * HEAD], start=True, stop=True)
            nc.vector.tensor_copy(out=gains[:], in_=gain_ps[:, 0 : 2 * HEAD])
            build_tables(nc.vector, gain_ps[:, 0 : 2 * HEAD], 0, VECTOR_TABLES)
            for j0 in range(VECTOR_TABLES, POS_TILES, 2):
                build_tables(nc.gpsimd, gains[:], j0, j0 + 2)

        prod = {}
        sumsq = {}
        rstd = {}

        def fused(t, n):
            return n >= FIRST_FUSED or t >= TOKEN_TILES - 2

        def project(t, n):
            c = t // CHUNK_TILES
            r = t % CHUNK_TILES
            acc = psum.tile([P, N_TILE], F32, name="acc", bufs=ACC_BUFS)
            for g in range(PASSES):
                nc.tensor.matmul_mx(
                    out=acc[:],
                    lhsT=x_codes[c][:, g, 2 * r * P : 2 * (r + 1) * P].bitcast(FP4X4),
                    lhsT_scale=x_planes[c][:, g, r * P : (r + 1) * P],
                    rhs=w_codes[n][:, g, :].bitcast(FP4X4),
                    rhs_scale=w_plane(n, g),
                    start=(g == 0),
                    stop=(g == PASSES - 1),
                )
            return acc

        def squares(t, n, acc):
            for h in range(HEADS_PER_BANK):
                junk = work.tile([P, HEAD], BF16, name="junk", bufs=4)
                col = n * HEADS_PER_BANK + h
                nc.scalar.activation(
                    out=junk[:], in_=acc[:, h * HEAD : (h + 1) * HEAD], func=ACT.Square,
                    accum_out=sumsq[t][:, col : col + 1],
                )

        def inv_norm(t, n0, n1):
            cols = slice(n0 * HEADS_PER_BANK, n1 * HEADS_PER_BANK)
            nc.scalar.activation(
                out=rstd[t][:, cols], in_=sumsq[t][:, cols], func=ACT.Abs_reciprocal_sqrt, scale=1.0 / HEAD, bias=EPS
            )

        def products(t, n, acc):
            j = t % POS_TILES
            which = 0 if n < Q_BANKS else 1
            table = tables[:, j, :, which * HEAD : (which + 1) * HEAD]
            if fused(t, n):
                for h in range(HEADS_PER_BANK):
                    col = n * HEADS_PER_BANK + h
                    nc.vector.scalar_tensor_tensor(
                        out=prod[t][:, :, col * HEAD : (col + 1) * HEAD],
                        in0=acc[:, h * HEAD : (h + 1) * HEAD].unsqueeze(1).to_broadcast([P, 2, HEAD]),
                        scalar=rstd[t][:, col : col + 1], in1=table, op0=ALU.mult, op1=ALU.mult,
                    )
            else:
                nc.vector.tensor_tensor(
                    out=prod[t][:, :, n * N_TILE : (n + 1) * N_TILE].rearrange("p s (h d) -> p s h d", d=HEAD),
                    in0=acc[:].rearrange("p (h d) -> p h d", d=HEAD).unsqueeze(1).to_broadcast([P, 2, HEADS_PER_BANK, HEAD]),
                    in1=table.unsqueeze(2).to_broadcast([P, 2, HEADS_PER_BANK, HEAD]),
                    op=ALU.mult,
                )

        def add_halves(eng, t, n0, n1):
            cols = slice(n0 * N_TILE, n1 * N_TILE)
            pc = prod[t][:, 0, cols].rearrange("p (h s i) -> p h s i", s=2, i=HALF)
            ps = prod[t][:, 1, cols].rearrange("p (h s i) -> p h s i", s=2, i=HALF)
            eng.tensor_tensor(out=pc, in0=pc, in1=ps[:, :, ::-1, :], op=ALU.add)

        def store(t, n):
            rows = slice(t * P, (t + 1) * P)
            cols = slice(n * N_TILE, (n + 1) * N_TILE)
            if n < Q_BANKS:
                nc.sync.dma_start(out=q_out[rows, cols], in_=prod[t][:, 0, cols])
            else:
                nc.sync.dma_start(out=k_out[rows, :], in_=prod[t][:, 0, cols])

        def finish(t, n):
            if not fused(t, n):
                for h in range(n * HEADS_PER_BANK, (n + 1) * HEADS_PER_BANK):
                    nc.scalar.activation(
                        out=prod[t][:, 0, h * HEAD : (h + 1) * HEAD], in_=prod[t][:, 0, h * HEAD : (h + 1) * HEAD],
                        func=ACT.Copy, scale=rstd[t][:, h : h + 1],
                    )
            store(t, n)

        def values(t, acc, queue):
            c = t // CHUNK_TILES
            r = t % CHUNK_TILES
            v_new = work.tile([P, N_TILE], F32, name="v_new", bufs=6, align_bytes=256)
            nc.vector.scalar_tensor_tensor(
                out=v_new[:], in0=v1_tiles[c][:, r, :], scalar=one_minus_lambda[:, 0:1], in1=acc[:],
                op0=ALU.mult, op1=ALU.add,
            )
            queue.dma_start(out=v_out[t * P : (t + 1) * P, :], in_=v_new[:])

        def lambda_column():
            nc.tensor.matmul(
                out=gain_ps[:, 2 * HEAD : 4 * HEAD], lhsT=ones[:], rhs=gain_row[:, 2 * HEAD : 4 * HEAD], start=True, stop=True
            )
            nc.vector.tensor_scalar(
                out=one_minus_lambda[:], in0=gain_ps[:, 2 * HEAD : 2 * HEAD + 1], scalar1=-1.0, scalar2=1.0,
                op0=ALU.mult, op1=ALU.add,
            )

        steps = []
        for t in range(EARLY_V):
            steps.append((t, V_BANK))
        for n in range(V_BANK):
            for t in range(FIRST_BLOCK):
                steps.append((t, n))
        woven = 0
        for t in range(FIRST_BLOCK, TOKEN_TILES):
            for n in range(V_BANK + 1):
                if n < V_BANK or (t not in HELD_V and t >= EARLY_V):
                    steps.append((t, n))
                for k in range(V_AFTER.get((t, n), 0)):
                    steps.append((HELD_V[woven], V_BANK))
                    woven += 1
        for t in HELD_V[woven:]:
            steps.append((t, V_BANK))

        to_scale = []
        to_store = []
        scaled = 0
        stored = 0
        banks = {}
        for i in range(len(steps) + 1):
            if i < len(steps):
                t, n = steps[i]
                if n == 0:
                    if t % CHUNK_TILES == 0 and t // CHUNK_TILES + 1 < CHUNKS:
                        c = t // CHUNK_TILES + 1
                        load_x_planes(c)
                        load_x_codes(c)
                        load_v1(c)
                    if t == 0:
                        for c in range(2, X_PLANE_BUFS):
                            fill_x_planes(c)
                    prod[t] = work.tile([P, 2, ROPE_COLS], F32, name="prod", bufs=PROD_BUFS, align_bytes=256)
                    sumsq[t] = work.tile([P, ROPE_HEADS], F32, name="sumsq", bufs=PROD_BUFS + 1)
                    rstd[t] = work.tile([P, ROPE_HEADS], F32, name="rstd", bufs=PROD_BUFS + 1)
                banks[i] = project(t, n)
                if i == 0:
                    lambda_column()
                if n < V_BANK:
                    squares(t, n, banks[i])
            if i == 0:
                continue
            t, n = steps[i - 1]
            if n == V_BANK:
                values(t, banks[i - 1], nc.scalar if i - 1 >= len(steps) - len(HELD_V) + woven else nc.sync)
            else:
                if fused(t, n):
                    inv_norm(t, n, n + 1)
                elif n == FIRST_FUSED - 1:
                    inv_norm(t, 0, FIRST_FUSED)
                products(t, n, banks[i - 1])
                for n0, n1 in TAIL_GROUPS.get(t, BODY_GROUPS):
                    if n == n1 - 1:
                        add_halves(nc.vector if (t, n0) in VECTOR_ADDS else nc.gpsimd, t, n0, n1)
                        early = EARLY_EXTRA if t < EARLY_TILES else 0
                        for nn in range(n0, n1):
                            if fused(t, nn):
                                to_store.append((i + STORE_DELAY + early, t, nn))
                            else:
                                to_scale.append((i + SCALE_DELAY + early, t, nn))
            if scaled < len(to_scale) and to_scale[scaled][0] <= i:
                finish(to_scale[scaled][1], to_scale[scaled][2])
                scaled += 1
            for k in range(2):
                if stored < len(to_store) and to_store[stored][0] <= i:
                    finish(to_store[stored][1], to_store[stored][2])
                    stored += 1
            if i == 1:
                gains_and_tables()
        while scaled < len(to_scale):
            finish(to_scale[scaled][1], to_scale[scaled][2])
            scaled += 1
        while stored < len(to_store):
            finish(to_store[stored][1], to_store[stored][2])
            stored += 1
